import numpy as np
import ml_dtypes


def mxq(x, axis, fmt="e4m3"):
    dtype, down = {"e4m3": (ml_dtypes.float8_e4m3fn, 7), "e5m2": (ml_dtypes.float8_e5m2, 14)}[fmt]
    v = np.moveaxis(np.asarray(x, np.float32).astype(ml_dtypes.bfloat16).astype(np.float64), axis, -1)
    blocks = v.reshape(v.shape[:-1] + (-1, 32))
    amax = np.abs(blocks).max(-1, keepdims=True)
    byte = np.maximum(np.where(amax > 0, np.frexp(amax)[1] - 1 + 127, 0) - down, 1)
    scale = np.exp2(byte - 127.0)
    codes = (blocks / scale).astype(np.float32).astype(dtype).astype(np.float64)
    return np.moveaxis((codes * scale).reshape(v.shape), -1, axis)


WIDE = False


def mx_kscale(k):
    if not WIDE:
        return np.ones(k)
    levels = np.array([10, -10, 5, -5, 0])
    a = np.random.permutation(np.resize(levels, k // 512 * 4)).reshape(k // 512, 4)
    idx = np.arange(k)
    return np.exp2(a[idx // 512, idx % 128 // 32])


BF16 = ml_dtypes.bfloat16


def bf(x):
    return np.asarray(x, np.float32).astype(BF16)


def f64(x):
    return np.asarray(x).astype(np.float64)


B, D, H = 512, 1024, 1024
PASS = 512
MX_REC = H % PASS == 0


def sigmoid(v):
    return 1.0 / (1.0 + np.exp(-v))


def setup_inputs():
    s = mx_kscale(D)
    r = mx_kscale(H) if MX_REC else np.ones(H)
    gate_b = np.concatenate([np.zeros(H), np.zeros(H), np.ones(H), np.zeros(H)])
    return {"x_t": bf(np.random.standard_normal((B, D)) * s),
            "h_prev": bf(np.random.standard_normal((B, H)) * r),
            "c_prev": bf(np.random.standard_normal((B, H))),
            "n_prev": bf(0.5 + np.abs(np.random.standard_normal((B, H)))),
            "W": bf(np.random.standard_normal((D, 4 * H)) / np.sqrt(D) / s[:, None]),
            "R": bf(np.random.standard_normal((H, 4 * H)) / np.sqrt(H) / r[:, None]),
            "b": bf(gate_b + 0.2 * np.random.standard_normal(4 * H))}


def reference(x_t, h_prev, c_prev, n_prev, W, R, b):
    inp = mxq(f64(x_t), 1, "e4m3") @ mxq(f64(W), 0, "e4m3")
    if MX_REC:
        rec = mxq(f64(h_prev), 1, "e4m3") @ mxq(f64(R), 0, "e4m3")
    else:
        rec = f64(h_prev) @ f64(R)
    pre = inp + rec + f64(b)
    z_tilde, i_tilde, f_tilde, o_tilde = np.split(pre, 4, axis=-1)
    z_t = np.tanh(z_tilde)
    i_t = np.minimum(np.exp(i_tilde), 50.0)
    f_t = sigmoid(f_tilde)
    o_t = sigmoid(o_tilde)
    c_t = f_t * f64(c_prev) + i_t * z_t
    n_t = f_t * f64(n_prev) + i_t
    h_t = o_t * (c_t / (n_t + 1e-6))
    return h_t, c_t, n_t

@@ -1,0 +1,300 @@
+from contextlib import ExitStack
+
+import concourse.mybir as mybir
+from concourse.masks import make_identity
+
+F32 = mybir.dt.float32
+BF16 = mybir.dt.bfloat16
+U32 = mybir.dt.uint32
+U8 = mybir.dt.uint8
+FP8X4 = mybir.dt.float8_e4m3fn_x4
+ACT = mybir.ActivationFunctionType
+ALU = mybir.AluOpType
+
+P = 128
+B = 512
+H = 1024
+HW = 512
+BT = 4
+NPASS = 4
+GZ, GI, GF, GO = 0, 1, 2, 3
+ORDER = (GF, GI, GZ, GO)
+EPS = 1e-6
+FLOPS = 2 * 512 * 2048 * 4096
+
+WA = (192, 384, 160, 320, 352, 320, 64, 128)
+RAW_BUFS = 8
+
+
+def tile_slstmcell_kernel(tc, x_t, h_prev, c_prev, n_prev, W, R, b, out_0, out_1, out_2):
+    nc = tc.nc
+    with ExitStack() as ctx:
+        const = ctx.enter_context(tc.tile_pool(name="const", bufs=1))
+        big = ctx.enter_context(tc.tile_pool(name="big", bufs=5))
+        gxp = ctx.enter_context(tc.tile_pool(name="gxp", bufs=2))
+        rawp = ctx.enter_context(tc.tile_pool(name="rawp", bufs=RAW_BUFS))
+        grp = ctx.enter_context(tc.tile_pool(name="grp", bufs=4))
+        wqp = ctx.enter_context(tc.tile_pool(name="wqp", bufs=4))
+        gtp = ctx.enter_context(tc.tile_pool(name="gtp", bufs=6))
+        accp = ctx.enter_context(tc.psum_pool(name="accp", bufs=4))
+        tpp = ctx.enter_context(tc.psum_pool(name="tpp", bufs=4))
+
+        ident = const.tile([P, P], F32, name="ident")
+        make_identity(nc, ident[:])
+        braw = const.tile([P, P], BF16, name="braw")
+        nc.vector.memset(braw[:], 0.0)
+        nc.scalar.dma_start(out=braw[0:32, :], in_=b.rearrange("(r c) -> r c", c=P))
+        bias_sb = const.tile([P, 32], F32, name="bias_sb")
+
+        xq = const.tile([P, NPASS, B], U32, name="xq", align_bytes=64)
+        xs = const.tile([P, NPASS, B], U8, name="xs", align_bytes=64)
+        cprev = const.tile([P, BT, H], BF16, name="cprev")
+        nprev = const.tile([P, BT, H], BF16, name="nprev")
+
+        xh = big.tile([P, 2, BT, H], BF16, name="xh", tag="big")
+        xh_w = xh[:].bitcast(F32)
+
+        raws = {}
+        grouped = {}
+        wq = {}
+        ws = {}
+
+        def load_unit(r):
+            q, c = r // NPASS, r % NPASS
+            g, half = ORDER[q // 2], q % 2
+            src = W if c < 2 else R
+            r0 = 512 * (c % 2)
+            c0 = g * H + half * HW
+            raw = rawp.tile([P, 4, HW], BF16, name="raw", tag="raw")
+            nc.sync.dma_start(
+                out=raw[:], in_=src[r0 : r0 + 512, c0 : c0 + HW].rearrange("(p j) w -> p j w", j=4)
+            )
+            raws[r] = raw
+
+        def regroup(r):
+            wa = WA[r // NPASS]
+            raw = raws[r]
+            gr = grp.tile([P, HW, 4], BF16, name="gr", tag="gr", align_bytes=64)
+            grouped[r] = gr
+            if wa > 0:
+                nc.vector.tensor_copy(
+                    out=gr[:, 0:wa, :].rearrange("p (c i) t -> p c t i", i=4),
+                    in_=raw[:, :, 0:wa].rearrange("p t (c i) -> p c t i", i=4),
+                )
+            if wa < HW:
+                nc.scalar.copy(
+                    out=gr[:, wa:HW, :].rearrange("p (c i) t -> p c t i", i=4),
+                    in_=raw[:, :, wa:HW].rearrange("p t (c i) -> p c t i", i=4),
+                )
+
+        def quant(r):
+            q, c = r // NPASS, r % NPASS
+            if c == 0:
+                wq[q] = wqp.tile([P, NPASS, HW], U32, name="wq", tag="wq", align_bytes=64)
+                ws[q] = wqp.tile([P, NPASS, HW], U8, name="ws", tag="ws", align_bytes=64)
+            nc.vector.quantize_mx(
+                out=wq[q][:, c, :].bitcast(FP8X4),
+                scales=ws[q][:, c, :],
+                in_=grouped[r][:].rearrange("p w t -> p (w t)"),
+            )
+
+        def x_prep(c):
+            s, half = c // 2, c % 2
+            gx = gxp.tile([P, B, 4], BF16, name="gx", tag="gx", align_bytes=64)
+            gx_w = gx[:].bitcast(F32)
+            for pair in range(2):
+                xt = tpp.tile([P, 2, 256], F32, name="xt", tag="tp")
+                for bl in range(2):
+                    bt = 2 * pair + bl
+                    words = xh_w[:, s, bt, 256 * half : 256 * half + 256].rearrange("p (q u) -> p q u", u=2)
+                    for u in range(2):
+                        nc.tensor.transpose(
+                            out=xt[:, u, bl * P : (bl + 1) * P], in_=words[:, :, u], identity=ident[:]
+                        )
+                nc.scalar.copy(
+                    out=gx_w[:, 256 * pair : 256 * pair + 256, :], in_=xt[:].rearrange("q u n -> q n u")
+                )
+            nc.vector.quantize_mx(
+                out=xq[:, c, :].bitcast(FP8X4), scales=xs[:, c, :], in_=gx[:].rearrange("p n t -> p (n t)")
+            )
+
+        def bias_prep():
+            bf32 = const.tile([P, P], F32, name="bf32")
+            nc.vector.tensor_copy(out=bf32[:], in_=braw[:])
+            pb = tpp.tile([P, BT, P], F32, name="pb", tag="tp")
+            nc.tensor.transpose(out=pb[:, 0, :], in_=bf32[:], identity=ident[:])
+            nc.vector.tensor_copy(out=bias_sb[:, 0:24], in_=pb[:, 0, 0:24])
+            nc.vector.tensor_scalar(
+                out=bias_sb[:, 24:32], in0=pb[:, 0, 24:32], scalar1=0.5, scalar2=None, op0=ALU.mult
+            )
+
+        accs = {}
+
+        def mm_pass(t, c):
+            q, jl = t // 4, t % 4
+            if c == 0:
+                accs[t] = accp.tile([P, B], F32, name="acc", tag="acc")
+            nc.tensor.matmul_mx(
+                out=accs[t][:],
+                lhsT=wq[q][:, c, jl * P : (jl + 1) * P].bitcast(FP8X4),
+                lhsT_scale=ws[q][:, c, jl * P : (jl + 1) * P],
+                rhs=xq[:, c, :].bitcast(FP8X4),
+                rhs_scale=xs[:, c, :],
+                start=(c == 0),
+                stop=(c == NPASS - 1),
+            )
+
+        FUNC = {GZ: ACT.Tanh, GI: ACT.Exp, GF: ACT.Sigmoid, GO: ACT.Tanh}
+
+        def gate_act(t, out_ap):
+            g, j = ORDER[t // 8], t % 8
+            col = g * 8 + j
+            nc.scalar.activation(
+                out=out_ap,
+                in_=accs[t][:],
+                func=FUNC[g],
+                bias=bias_sb[:, col : col + 1],
+                scale=(0.5 if g == GO else 1.0),
+            )
+
+        def back(src_ap):
+            ps = tpp.tile([P, BT, P], F32, name="ps", tag="tp")
+            for bt in range(BT):
+                nc.tensor.transpose(out=ps[:, bt, :], in_=src_ap[:, bt * P : (bt + 1) * P], identity=ident[:])
+            return ps
+
+        o_h = out_0.rearrange("(p t) h -> p t h", t=BT)
+        o_c = out_1.rearrange("(p t) h -> p t h", t=BT)
+        o_n = out_2.rearrange("(p t) h -> p t h", t=BT)
+
+        def cols(j):
+            return slice(j * P, (j + 1) * P)
+
+        def halfcols(h):
+            return slice(h * HW, (h + 1) * HW)
+
+        load_unit(0)
+        load_unit(1)
+        nc.sync.dma_start(out=xh[:, 0], in_=x_t.rearrange("(p t) k -> p t k", t=BT))
+        load_unit(2)
+        load_unit(3)
+        nc.sync.dma_start(out=xh[:, 1], in_=h_prev.rearrange("(p t) k -> p t k", t=BT))
+        for r in range(4, RAW_BUFS):
+            load_unit(r)
+        nc.sync.dma_start(out=cprev[:], in_=c_prev.rearrange("(p t) h -> p t h", t=BT))
+        nc.sync.dma_start(out=nprev[:], in_=n_prev.rearrange("(p t) h -> p t h", t=BT))
+        bias_prep()
+
+        cc = big.tile([P, BT, H], F32, name="cc", tag="big")
+        nn = big.tile([P, BT, H], F32, name="nn", tag="big")
+        eT = big.tile([P, 8, B], F32, name="eT", tag="big")
+        late = {}
+
+        gts = {}
+
+        def front(t):
+            g = ORDER[t // 8]
+            if t < 28:
+                for c in range(NPASS):
+                    mm_pass(t, c)
+            if g == GI:
+                gts[t] = eT[:, t % 8, :]
+            else:
+                gT = gtp.tile([P, B], F32, name="gT", tag="gT")
+                gts[t] = gT[:]
+            gate_act(t, gts[t])
+
+        def rear(t):
+            g, j = ORDER[t // 8], t % 8
+            js = cols(j)
+            if g == GZ:
+                nc.vector.scalar_tensor_tensor(
+                    out=gts[t], in0=eT[:, j, :], scalar=50.0, in1=gts[t], op0=ALU.min, op1=ALU.mult
+                )
+            ps = back(gts[t])
+            if g == GF:
+                nc.vector.tensor_tensor(out=cc[:, :, js], in0=ps[:], in1=cprev[:, :, js], op=ALU.mult)
+                nc.vector.tensor_tensor(out=nn[:, :, js], in0=ps[:], in1=nprev[:, :, js], op=ALU.mult)
+            elif g == GI:
+                nc.vector.scalar_tensor_tensor(
+                    out=nn[:, :, js], in0=ps[:], scalar=50.0, in1=nn[:, :, js], op0=ALU.min, op1=ALU.add
+                )
+            elif g == GZ:
+                nc.vector.tensor_tensor(out=cc[:, :, js], in0=ps[:], in1=cc[:, :, js], op=ALU.add)
+                nc.vector.tensor_tensor(
+                    out=late["hh"][:, :, js], in0=cc[:, :, js], in1=late["sq"][:, :, js], op=ALU.mult
+                )
+            else:
+                nc.vector.scalar_tensor_tensor(
+                    out=late["hh"][:, :, js], in0=ps[:], scalar=1.0, in1=late["hh"][:, :, js], op0=ALU.add, op1=ALU.mult
+                )
+
+        state = {"next_load": RAW_BUFS}
+
+        for q in range(8):
+            g, half = ORDER[q // 2], q % 2
+            for c in range(NPASS):
+                r = NPASS * q + c
+                regroup(r)
+                if state["next_load"] < 32:
+                    load_unit(state["next_load"])
+                    state["next_load"] += 1
+                if c > 0:
+                    quant(r - 1)
+                    if q == 7:
+                        for t in range(28, 32):
+                            mm_pass(t, c - 1)
+                if q == 0 and c == 1:
+                    x_prep(0)
+                if q == 0 and c == 2:
+                    x_prep(1)
+                if q == 0 and c == 3:
+                    x_prep(2)
+                    x_prep(3)
+            quant(NPASS * q + 3)
+            if q == 7:
+                for t in range(28, 32):
+                    mm_pass(t, 3)
+            tiles = [4 * q + jl for jl in range(4)]
+            front(tiles[0])
+            front(tiles[1])
+            for jl in range(4):
+                if jl + 2 < 4:
+                    front(tiles[jl + 2])
+                rear(tiles[jl])
+                if g == GO and jl % 2 == 1:
+                    j = tiles[jl] % 8
+                    hs = slice((j - 1) * P, (j + 1) * P)
+                    nc.gpsimd.dma_start(out=o_h[:, :, hs], in_=late["hh"][:, :, hs])
+            hs = halfcols(half)
+            if g == GI:
+                nc.gpsimd.dma_start(out=o_n[:, :, hs], in_=nn[:, :, hs])
+                if half == 1:
+                    late["sq"] = big.tile([P, BT, H], F32, name="sq", tag="big")
+                    late["sg"] = big.tile([P, BT, H], F32, name="sg", tag="big")
+                    sq, sg = late["sq"], late["sg"]
+                    for h in range(2):
+                        nc.scalar.activation(
+                            out=sq[:, :, halfcols(h)],
+                            in_=nn[:, :, halfcols(h)],
+                            func=ACT.Abs_reciprocal_sqrt,
+                            bias=EPS,
+                            scale=1.0,
+                        )
+                    for h in range(2):
+                        nc.vector.tensor_scalar(
+                            out=sg[:, :, halfcols(h)],
+                            in0=nn[:, :, halfcols(h)],
+                            scalar1=-EPS,
+                            scalar2=0.5,
+                            op0=ALU.is_ge,
+                            op1=ALU.subtract,
+                        )
+                        nc.scalar.activation(out=sq[:, :, halfcols(h)], in_=sq[:, :, halfcols(h)], func=ACT.Square)
+                    for h in range(2):
+                        nc.vector.tensor_tensor(
+                            out=sq[:, :, halfcols(h)], in0=sq[:, :, halfcols(h)], in1=sg[:, :, halfcols(h)], op=ALU.mult
+                        )
+                    late["hh"] = big.tile([P, BT, H], F32, name="hh", tag="big")
+            if g == GZ:
+                nc.gpsimd.dma_start(out=o_c[:, :, hs], in_=cc[:, :, hs])

@@ -22,7 +22,7 @@ ORDER = (GF, GI, GZ, GO)
 EPS = 1e-6
 FLOPS = 2 * 512 * 2048 * 4096
 
-WA = (192, 384, 160, 320, 352, 320, 64, 128)
+WA = (256, 384, 192, 352, 320, 448, 32, 96)
 RAW_BUFS = 8
 
 
@@ -35,7 +35,7 @@ def tile_slstmcell_kernel(tc, x_t, h_prev, c_prev, n_prev, W, R, b, out_0, out_1
         rawp = ctx.enter_context(tc.tile_pool(name="rawp", bufs=RAW_BUFS))
         grp = ctx.enter_context(tc.tile_pool(name="grp", bufs=4))
         wqp = ctx.enter_context(tc.tile_pool(name="wqp", bufs=4))
-        gtp = ctx.enter_context(tc.tile_pool(name="gtp", bufs=6))
+        gtp = ctx.enter_context(tc.tile_pool(name="gtp", bufs=12))
         accp = ctx.enter_context(tc.psum_pool(name="accp", bufs=4))
         tpp = ctx.enter_context(tc.psum_pool(name="tpp", bufs=4))
 
@@ -45,6 +45,9 @@ def tile_slstmcell_kernel(tc, x_t, h_prev, c_prev, n_prev, W, R, b, out_0, out_1
         nc.vector.memset(braw[:], 0.0)
         nc.scalar.dma_start(out=braw[0:32, :], in_=b.rearrange("(r c) -> r c", c=P))
         bias_sb = const.tile([P, 32], F32, name="bias_sb")
+        warm = const.tile([P, 1], F32, name="warm")
+        nc.vector.memset(warm[:], 0.0)
+        nc.scalar.activation(out=warm[:], in_=warm[:], func=ACT.Sigmoid)
 
         xq = const.tile([P, NPASS, B], U32, name="xq", align_bytes=64)
         xs = const.tile([P, NPASS, B], U8, name="xs", align_bytes=64)
@@ -183,7 +186,6 @@ def tile_slstmcell_kernel(tc, x_t, h_prev, c_prev, n_prev, W, R, b, out_0, out_1
             load_unit(r)
         nc.sync.dma_start(out=cprev[:], in_=c_prev.rearrange("(p t) h -> p t h", t=BT))
         nc.sync.dma_start(out=nprev[:], in_=n_prev.rearrange("(p t) h -> p t h", t=BT))
-        bias_prep()
 
         cc = big.tile([P, BT, H], F32, name="cc", tag="big")
         nn = big.tile([P, BT, H], F32, name="nn", tag="big")
@@ -191,110 +193,107 @@ def tile_slstmcell_kernel(tc, x_t, h_prev, c_prev, n_prev, W, R, b, out_0, out_1
         late = {}
 
         gts = {}
-
-        def front(t):
-            g = ORDER[t // 8]
-            if t < 28:
-                for c in range(NPASS):
-                    mm_pass(t, c)
-            if g == GI:
-                gts[t] = eT[:, t % 8, :]
-            else:
-                gT = gtp.tile([P, B], F32, name="gT", tag="gT")
-                gts[t] = gT[:]
-            gate_act(t, gts[t])
-
-        def rear(t):
-            g, j = ORDER[t // 8], t % 8
-            js = cols(j)
-            if g == GZ:
-                nc.vector.scalar_tensor_tensor(
-                    out=gts[t], in0=eT[:, j, :], scalar=50.0, in1=gts[t], op0=ALU.min, op1=ALU.mult
-                )
-            ps = back(gts[t])
-            if g == GF:
-                nc.vector.tensor_tensor(out=cc[:, :, js], in0=ps[:], in1=cprev[:, :, js], op=ALU.mult)
-                nc.vector.tensor_tensor(out=nn[:, :, js], in0=ps[:], in1=nprev[:, :, js], op=ALU.mult)
-            elif g == GI:
-                nc.vector.scalar_tensor_tensor(
-                    out=nn[:, :, js], in0=ps[:], scalar=50.0, in1=nn[:, :, js], op0=ALU.min, op1=ALU.add
-                )
-            elif g == GZ:
-                nc.vector.tensor_tensor(out=cc[:, :, js], in0=ps[:], in1=cc[:, :, js], op=ALU.add)
-                nc.vector.tensor_tensor(
-                    out=late["hh"][:, :, js], in0=cc[:, :, js], in1=late["sq"][:, :, js], op=ALU.mult
-                )
-            else:
-                nc.vector.scalar_tensor_tensor(
-                    out=late["hh"][:, :, js], in0=ps[:], scalar=1.0, in1=late["hh"][:, :, js], op0=ALU.add, op1=ALU.mult
-                )
-
         state = {"next_load": RAW_BUFS}
 
-        for q in range(8):
-            g, half = ORDER[q // 2], q % 2
-            for c in range(NPASS):
+        def rq(q):
+            for c in range(NPASS + 1):
                 r = NPASS * q + c
-                regroup(r)
-                if state["next_load"] < 32:
-                    load_unit(state["next_load"])
-                    state["next_load"] += 1
+                if c < NPASS:
+                    regroup(r)
+                    if state["next_load"] < 32:
+                        load_unit(state["next_load"])
+                        state["next_load"] += 1
                 if c > 0:
                     quant(r - 1)
-                    if q == 7:
-                        for t in range(28, 32):
-                            mm_pass(t, c - 1)
-                if q == 0 and c == 1:
-                    x_prep(0)
-                if q == 0 and c == 2:
-                    x_prep(1)
-                if q == 0 and c == 3:
-                    x_prep(2)
-                    x_prep(3)
-            quant(NPASS * q + 3)
-            if q == 7:
-                for t in range(28, 32):
-                    mm_pass(t, 3)
-            tiles = [4 * q + jl for jl in range(4)]
-            front(tiles[0])
-            front(tiles[1])
-            for jl in range(4):
-                if jl + 2 < 4:
-                    front(tiles[jl + 2])
-                rear(tiles[jl])
-                if g == GO and jl % 2 == 1:
-                    j = tiles[jl] % 8
-                    hs = slice((j - 1) * P, (j + 1) * P)
-                    nc.gpsimd.dma_start(out=o_h[:, :, hs], in_=late["hh"][:, :, hs])
+                    if q == 0:
+                        x_prep(c - 1)
+                    for t in range(4 * q, 4 * q + 4):
+                        mm_pass(t, c - 1)
+
+        def front(q):
+            for t in range(4 * q, 4 * q + 4):
+                if ORDER[t // 8] == GI:
+                    gts[t] = eT[:, t % 8, :]
+                else:
+                    gT = gtp.tile([P, B], F32, name="gT", tag="gT")
+                    gts[t] = gT[:]
+                gate_act(t, gts[t])
+
+        def recip():
+            late["sq"] = big.tile([P, BT, H], F32, name="sq", tag="big")
+            late["sg"] = big.tile([P, BT, H], F32, name="sg", tag="big")
+            sq, sg = late["sq"], late["sg"]
+            for h in range(2):
+                nc.scalar.activation(
+                    out=sq[:, :, halfcols(h)],
+                    in_=nn[:, :, halfcols(h)],
+                    func=ACT.Abs_reciprocal_sqrt,
+                    bias=EPS,
+                    scale=1.0,
+                )
+            for h in range(2):
+                nc.vector.tensor_scalar(
+                    out=sg[:, :, halfcols(h)],
+                    in0=nn[:, :, halfcols(h)],
+                    scalar1=-EPS,
+                    scalar2=0.5,
+                    op0=ALU.is_ge,
+                    op1=ALU.subtract,
+                )
+                nc.scalar.activation(out=sq[:, :, halfcols(h)], in_=sq[:, :, halfcols(h)], func=ACT.Square)
+            for h in range(2):
+                nc.vector.tensor_tensor(
+                    out=sq[:, :, halfcols(h)], in0=sq[:, :, halfcols(h)], in1=sg[:, :, halfcols(h)], op=ALU.mult
+                )
+            late["hh"] = big.tile([P, BT, H], F32, name="hh", tag="big")
+
+        def rear(q):
+            g, half = ORDER[q // 2], q % 2
+            for t in range(4 * q, 4 * q + 4):
+                j = t % 8
+                js = cols(j)
+                if g == GZ:
+                    nc.vector.scalar_tensor_tensor(
+                        out=gts[t], in0=eT[:, j, :], scalar=50.0, in1=gts[t], op0=ALU.min, op1=ALU.mult
+                    )
+                ps = back(gts[t])
+                if g == GF:
+                    nc.vector.tensor_tensor(out=cc[:, :, js], in0=ps[:], in1=cprev[:, :, js], op=ALU.mult)
+                    nc.vector.tensor_tensor(out=nn[:, :, js], in0=ps[:], in1=nprev[:, :, js], op=ALU.mult)
+                elif g == GI:
+                    nc.vector.scalar_tensor_tensor(
+                        out=nn[:, :, js], in0=ps[:], scalar=50.0, in1=nn[:, :, js], op0=ALU.min, op1=ALU.add
+                    )
+                elif g == GZ:
+                    nc.vector.tensor_tensor(out=cc[:, :, js], in0=ps[:], in1=cc[:, :, js], op=ALU.add)
+                    nc.vector.tensor_tensor(
+                        out=late["hh"][:, :, js], in0=cc[:, :, js], in1=late["sq"][:, :, js], op=ALU.mult
+                    )
+                else:
+                    nc.vector.scalar_tensor_tensor(
+                        out=late["hh"][:, :, js], in0=ps[:], scalar=1.0, in1=late["hh"][:, :, js], op0=ALU.add, op1=ALU.mult
+                    )
+                    if j >= 6:
+                        nc.sync.dma_start(out=o_h[:, :, js], in_=late["hh"][:, :, js])
+                    elif j % 2 == 1:
+                        hs = slice((j - 1) * P, (j + 1) * P)
+                        nc.sync.dma_start(out=o_h[:, :, hs], in_=late["hh"][:, :, hs])
             hs = halfcols(half)
             if g == GI:
                 nc.gpsimd.dma_start(out=o_n[:, :, hs], in_=nn[:, :, hs])
                 if half == 1:
-                    late["sq"] = big.tile([P, BT, H], F32, name="sq", tag="big")
-                    late["sg"] = big.tile([P, BT, H], F32, name="sg", tag="big")
-                    sq, sg = late["sq"], late["sg"]
-                    for h in range(2):
-                        nc.scalar.activation(
-                            out=sq[:, :, halfcols(h)],
-                            in_=nn[:, :, halfcols(h)],
-                            func=ACT.Abs_reciprocal_sqrt,
-                            bias=EPS,
-                            scale=1.0,
-                        )
-                    for h in range(2):
-                        nc.vector.tensor_scalar(
-                            out=sg[:, :, halfcols(h)],
-                            in0=nn[:, :, halfcols(h)],
-                            scalar1=-EPS,
-                            scalar2=0.5,
-                            op0=ALU.is_ge,
-                            op1=ALU.subtract,
-                        )
-                        nc.scalar.activation(out=sq[:, :, halfcols(h)], in_=sq[:, :, halfcols(h)], func=ACT.Square)
-                    for h in range(2):
-                        nc.vector.tensor_tensor(
-                            out=sq[:, :, halfcols(h)], in0=sq[:, :, halfcols(h)], in1=sg[:, :, halfcols(h)], op=ALU.mult
-                        )
-                    late["hh"] = big.tile([P, BT, H], F32, name="hh", tag="big")
+                    recip()
             if g == GZ:
                 nc.gpsimd.dma_start(out=o_c[:, :, hs], in_=cc[:, :, hs])
+
+        for q in range(5):
+            rq(q)
+            if q == 0:
+                bias_prep()
+            front(q)
+            rear(q)
+        for q in range(5, 8):
+            rq(q)
+            front(q)
+        for q in range(5, 8):
+            rear(q)

@@ -22,7 +22,7 @@ ORDER = (GF, GI, GZ, GO)
 EPS = 1e-6
 FLOPS = 2 * 512 * 2048 * 4096
 
-WA = (256, 384, 192, 352, 320, 448, 32, 96)
+WA = (256, 416, 192, 352, 352, 512, 32, 96)
 RAW_BUFS = 8
 
 

@@ -22,7 +22,7 @@ ORDER = (GF, GI, GZ, GO)
 EPS = 1e-6
 FLOPS = 2 * 512 * 2048 * 4096
 
-WA = (256, 416, 192, 352, 352, 512, 32, 96)
+WA = (256, 320, 160, 320, 352, 512, 32, 128)
 RAW_BUFS = 8
 
 
@@ -35,7 +35,7 @@ def tile_slstmcell_kernel(tc, x_t, h_prev, c_prev, n_prev, W, R, b, out_0, out_1
         rawp = ctx.enter_context(tc.tile_pool(name="rawp", bufs=RAW_BUFS))
         grp = ctx.enter_context(tc.tile_pool(name="grp", bufs=4))
         wqp = ctx.enter_context(tc.tile_pool(name="wqp", bufs=4))
-        gtp = ctx.enter_context(tc.tile_pool(name="gtp", bufs=12))
+        gtp = ctx.enter_context(tc.tile_pool(name="gtp", bufs=3))
         accp = ctx.enter_context(tc.psum_pool(name="accp", bufs=4))
         tpp = ctx.enter_context(tc.psum_pool(name="tpp", bufs=4))
 
@@ -211,13 +211,19 @@ def tile_slstmcell_kernel(tc, x_t, h_prev, c_prev, n_prev, W, R, b, out_0, out_1
                         mm_pass(t, c - 1)
 
         def front(q):
+            g, half = ORDER[q // 2], q % 2
+            if g != GI:
+                gT = gtp.tile([P, 4, B], F32, name="gT", tag="gT")
             for t in range(4 * q, 4 * q + 4):
-                if ORDER[t // 8] == GI:
+                if g == GI:
                     gts[t] = eT[:, t % 8, :]
                 else:
-                    gT = gtp.tile([P, B], F32, name="gT", tag="gT")
-                    gts[t] = gT[:]
+                    gts[t] = gT[:, t % 4, :]
                 gate_act(t, gts[t])
+            if g == GZ:
+                nc.vector.scalar_tensor_tensor(
+                    out=gT[:], in0=eT[:, 4 * half : 4 * half + 4, :], scalar=50.0, in1=gT[:], op0=ALU.min, op1=ALU.mult
+                )
 
         def recip():
             late["sq"] = big.tile([P, BT, H], F32, name="sq", tag="big")
@@ -252,10 +258,6 @@ def tile_slstmcell_kernel(tc, x_t, h_prev, c_prev, n_prev, W, R, b, out_0, out_1
             for t in range(4 * q, 4 * q + 4):
                 j = t % 8
                 js = cols(j)
-                if g == GZ:
-                    nc.vector.scalar_tensor_tensor(
-                        out=gts[t], in0=eT[:, j, :], scalar=50.0, in1=gts[t], op0=ALU.min, op1=ALU.mult
-                    )
                 ps = back(gts[t])
                 if g == GF:
                     nc.vector.tensor_tensor(out=cc[:, :, js], in0=ps[:], in1=cprev[:, :, js], op=ALU.mult)
@@ -266,9 +268,6 @@ def tile_slstmcell_kernel(tc, x_t, h_prev, c_prev, n_prev, W, R, b, out_0, out_1
                     )
                 elif g == GZ:
                     nc.vector.tensor_tensor(out=cc[:, :, js], in0=ps[:], in1=cc[:, :, js], op=ALU.add)
-                    nc.vector.tensor_tensor(
-                        out=late["hh"][:, :, js], in0=cc[:, :, js], in1=late["sq"][:, :, js], op=ALU.mult
-                    )
                 else:
                     nc.vector.scalar_tensor_tensor(
                         out=late["hh"][:, :, js], in0=ps[:], scalar=1.0, in1=late["hh"][:, :, js], op0=ALU.add, op1=ALU.mult
@@ -285,6 +284,9 @@ def tile_slstmcell_kernel(tc, x_t, h_prev, c_prev, n_prev, W, R, b, out_0, out_1
                     recip()
             if g == GZ:
                 nc.gpsimd.dma_start(out=o_c[:, :, hs], in_=cc[:, :, hs])
+                nc.vector.tensor_tensor(
+                    out=late["hh"][:, :, hs], in0=cc[:, :, hs], in1=late["sq"][:, :, hs], op=ALU.mult
+                )
 
         for q in range(5):
             rq(q)

@@ -30,7 +30,7 @@ def tile_slstmcell_kernel(tc, x_t, h_prev, c_prev, n_prev, W, R, b, out_0, out_1
     nc = tc.nc
     with ExitStack() as ctx:
         const = ctx.enter_context(tc.tile_pool(name="const", bufs=1))
-        big = ctx.enter_context(tc.tile_pool(name="big", bufs=5))
+        big = ctx.enter_context(tc.tile_pool(name="big", bufs=3))
         gxp = ctx.enter_context(tc.tile_pool(name="gxp", bufs=2))
         rawp = ctx.enter_context(tc.tile_pool(name="rawp", bufs=RAW_BUFS))
         grp = ctx.enter_context(tc.tile_pool(name="grp", bufs=4))
@@ -51,8 +51,8 @@ def tile_slstmcell_kernel(tc, x_t, h_prev, c_prev, n_prev, W, R, b, out_0, out_1
 
         xq = const.tile([P, NPASS, B], U32, name="xq", align_bytes=64)
         xs = const.tile([P, NPASS, B], U8, name="xs", align_bytes=64)
-        cprev = const.tile([P, BT, H], BF16, name="cprev")
-        nprev = const.tile([P, BT, H], BF16, name="nprev")
+        cn_prev = const.tile([P, 2, BT, H], BF16, name="cn_prev")
+        cn = const.tile([P, 2, BT, H], F32, name="cn")
 
         xh = big.tile([P, 2, BT, H], BF16, name="xh", tag="big")
         xh_w = xh[:].bitcast(F32)
@@ -184,11 +184,11 @@ def tile_slstmcell_kernel(tc, x_t, h_prev, c_prev, n_prev, W, R, b, out_0, out_1
         nc.sync.dma_start(out=xh[:, 1], in_=h_prev.rearrange("(p t) k -> p t k", t=BT))
         for r in range(4, RAW_BUFS):
             load_unit(r)
-        nc.sync.dma_start(out=cprev[:], in_=c_prev.rearrange("(p t) h -> p t h", t=BT))
-        nc.sync.dma_start(out=nprev[:], in_=n_prev.rearrange("(p t) h -> p t h", t=BT))
+        nc.sync.dma_start(out=cn_prev[:, 0], in_=c_prev.rearrange("(p t) h -> p t h", t=BT))
+        nc.sync.dma_start(out=cn_prev[:, 1], in_=n_prev.rearrange("(p t) h -> p t h", t=BT))
 
-        cc = big.tile([P, BT, H], F32, name="cc", tag="big")
-        nn = big.tile([P, BT, H], F32, name="nn", tag="big")
+        cc = cn[:, 0]
+        nn = cn[:, 1]
         eT = big.tile([P, 8, B], F32, name="eT", tag="big")
         late = {}
 
@@ -260,8 +260,12 @@ def tile_slstmcell_kernel(tc, x_t, h_prev, c_prev, n_prev, W, R, b, out_0, out_1
                 js = cols(j)
                 ps = back(gts[t])
                 if g == GF:
-                    nc.vector.tensor_tensor(out=cc[:, :, js], in0=ps[:], in1=cprev[:, :, js], op=ALU.mult)
-                    nc.vector.tensor_tensor(out=nn[:, :, js], in0=ps[:], in1=nprev[:, :, js], op=ALU.mult)
+                    nc.vector.tensor_tensor(
+                        out=cn[:, :, :, js],
+                        in0=ps[:].unsqueeze(1).to_broadcast([P, 2, BT, P]),
+                        in1=cn_prev[:, :, :, js],
+                        op=ALU.mult,
+                    )
                 elif g == GI:
                     nc.vector.scalar_tensor_tensor(
                         out=nn[:, :, js], in0=ps[:], scalar=50.0, in1=nn[:, :, js], op0=ALU.min, op1=ALU.add

@@ -30,7 +30,7 @@ def tile_slstmcell_kernel(tc, x_t, h_prev, c_prev, n_prev, W, R, b, out_0, out_1
     nc = tc.nc
     with ExitStack() as ctx:
         const = ctx.enter_context(tc.tile_pool(name="const", bufs=1))
-        big = ctx.enter_context(tc.tile_pool(name="big", bufs=3))
+        big = ctx.enter_context(tc.tile_pool(name="big", bufs=5))
         gxp = ctx.enter_context(tc.tile_pool(name="gxp", bufs=2))
         rawp = ctx.enter_context(tc.tile_pool(name="rawp", bufs=RAW_BUFS))
         grp = ctx.enter_context(tc.tile_pool(name="grp", bufs=4))
@@ -51,8 +51,8 @@ def tile_slstmcell_kernel(tc, x_t, h_prev, c_prev, n_prev, W, R, b, out_0, out_1
 
         xq = const.tile([P, NPASS, B], U32, name="xq", align_bytes=64)
         xs = const.tile([P, NPASS, B], U8, name="xs", align_bytes=64)
-        cn_prev = const.tile([P, 2, BT, H], BF16, name="cn_prev")
-        cn = const.tile([P, 2, BT, H], F32, name="cn")
+        cprev = const.tile([P, BT, H], BF16, name="cprev")
+        nprev = const.tile([P, BT, H], BF16, name="nprev")
 
         xh = big.tile([P, 2, BT, H], BF16, name="xh", tag="big")
         xh_w = xh[:].bitcast(F32)
@@ -184,11 +184,11 @@ def tile_slstmcell_kernel(tc, x_t, h_prev, c_prev, n_prev, W, R, b, out_0, out_1
         nc.sync.dma_start(out=xh[:, 1], in_=h_prev.rearrange("(p t) k -> p t k", t=BT))
         for r in range(4, RAW_BUFS):
             load_unit(r)
-        nc.sync.dma_start(out=cn_prev[:, 0], in_=c_prev.rearrange("(p t) h -> p t h", t=BT))
-        nc.sync.dma_start(out=cn_prev[:, 1], in_=n_prev.rearrange("(p t) h -> p t h", t=BT))
+        nc.sync.dma_start(out=cprev[:], in_=c_prev.rearrange("(p t) h -> p t h", t=BT))
+        nc.sync.dma_start(out=nprev[:], in_=n_prev.rearrange("(p t) h -> p t h", t=BT))
 
-        cc = cn[:, 0]
-        nn = cn[:, 1]
+        cc = big.tile([P, BT, H], F32, name="cc", tag="big")
+        nn = big.tile([P, BT, H], F32, name="nn", tag="big")
         eT = big.tile([P, 8, B], F32, name="eT", tag="big")
         late = {}
 
@@ -260,12 +260,8 @@ def tile_slstmcell_kernel(tc, x_t, h_prev, c_prev, n_prev, W, R, b, out_0, out_1
                 js = cols(j)
                 ps = back(gts[t])
                 if g == GF:
-                    nc.vector.tensor_tensor(
-                        out=cn[:, :, :, js],
-                        in0=ps[:].unsqueeze(1).to_broadcast([P, 2, BT, P]),
-                        in1=cn_prev[:, :, :, js],
-                        op=ALU.mult,
-                    )
+                    nc.vector.tensor_tensor(out=cc[:, :, js], in0=ps[:], in1=cprev[:, :, js], op=ALU.mult)
+                    nc.vector.tensor_tensor(out=nn[:, :, js], in0=ps[:], in1=nprev[:, :, js], op=ALU.mult)
                 elif g == GI:
                     nc.vector.scalar_tensor_tensor(
                         out=nn[:, :, js], in0=ps[:], scalar=50.0, in1=nn[:, :, js], op0=ALU.min, op1=ALU.add
@@ -283,11 +279,11 @@ def tile_slstmcell_kernel(tc, x_t, h_prev, c_prev, n_prev, W, R, b, out_0, out_1
                         nc.sync.dma_start(out=o_h[:, :, hs], in_=late["hh"][:, :, hs])
             hs = halfcols(half)
             if g == GI:
-                nc.gpsimd.dma_start(out=o_n[:, :, hs], in_=nn[:, :, hs])
+                nc.sync.dma_start(out=o_n[:, :, hs], in_=nn[:, :, hs])
                 if half == 1:
                     recip()
             if g == GZ:
-                nc.gpsimd.dma_start(out=o_c[:, :, hs], in_=cc[:, :, hs])
+                nc.sync.dma_start(out=o_c[:, :, hs], in_=cc[:, :, hs])
                 nc.vector.tensor_tensor(
                     out=late["hh"][:, :, hs], in0=cc[:, :, hs], in1=late["sq"][:, :, hs], op=ALU.mult
                 )

@@ -10,6 +10,7 @@ U8 = mybir.dt.uint8
 FP8X4 = mybir.dt.float8_e4m3fn_x4
 ACT = mybir.ActivationFunctionType
 ALU = mybir.AluOpType
+ENG = mybir.EngineType
 
 P = 128
 B = 512
@@ -17,13 +18,23 @@ H = 1024
 HW = 512
 BT = 4
 NPASS = 4
+NU = 32
 GZ, GI, GF, GO = 0, 1, 2, 3
 ORDER = (GF, GI, GZ, GO)
 EPS = 1e-6
 FLOPS = 2 * 512 * 2048 * 4096
 
-WA = (256, 320, 160, 320, 352, 512, 32, 128)
+WA = (256, 256, 32, 192, 352, 512, 0, 64)
+PW = (0, 0, 0, 0, 0, 0, 0, 0)
 RAW_BUFS = 8
+LI, LC, LDS = 3, 2, 2
+LP = 1
+XS = 1
+TPB = 4
+GRB = 6
+SQ = 3
+LP0 = 8
+GWF, GWO = 512, 288
 
 
 def tile_slstmcell_kernel(tc, x_t, h_prev, c_prev, n_prev, W, R, b, out_0, out_1, out_2):
@@ -33,14 +44,18 @@ def tile_slstmcell_kernel(tc, x_t, h_prev, c_prev, n_prev, W, R, b, out_0, out_1
         big = ctx.enter_context(tc.tile_pool(name="big", bufs=5))
         gxp = ctx.enter_context(tc.tile_pool(name="gxp", bufs=2))
         rawp = ctx.enter_context(tc.tile_pool(name="rawp", bufs=RAW_BUFS))
-        grp = ctx.enter_context(tc.tile_pool(name="grp", bufs=4))
-        wqp = ctx.enter_context(tc.tile_pool(name="wqp", bufs=4))
+        grp = ctx.enter_context(tc.tile_pool(name="grp", bufs=GRB))
+        ggp = ctx.enter_context(tc.tile_pool(name="ggp", bufs=1))
+        wqp = ctx.enter_context(tc.tile_pool(name="wqp", bufs=3))
         gtp = ctx.enter_context(tc.tile_pool(name="gtp", bufs=3))
         accp = ctx.enter_context(tc.psum_pool(name="accp", bufs=4))
-        tpp = ctx.enter_context(tc.psum_pool(name="tpp", bufs=4))
+        tpp = ctx.enter_context(tc.psum_pool(name="tpp", bufs=TPB))
+        ipp = ctx.enter_context(tc.psum_pool(name="ipp", bufs=4 - TPB)) if TPB < 4 else None
 
         ident = const.tile([P, P], F32, name="ident")
         make_identity(nc, ident[:])
+        identb = const.tile([P, P], BF16, name="identb")
+        make_identity(nc, identb[:])
         braw = const.tile([P, P], BF16, name="braw")
         nc.vector.memset(braw[:], 0.0)
         nc.scalar.dma_start(out=braw[0:32, :], in_=b.rearrange("(r c) -> r c", c=P))
@@ -58,7 +73,9 @@ def tile_slstmcell_kernel(tc, x_t, h_prev, c_prev, n_prev, W, R, b, out_0, out_1
         xh_w = xh[:].bitcast(F32)
 
         raws = {}
+        gw = {}
         grouped = {}
+        ips = {}
         wq = {}
         ws = {}
 
@@ -74,20 +91,62 @@ def tile_slstmcell_kernel(tc, x_t, h_prev, c_prev, n_prev, W, R, b, out_0, out_1
             )
             raws[r] = raw
 
-        def regroup(r):
-            wa = WA[r // NPASS]
-            raw = raws[r]
+        def pe_ident(r):
+            pw = PW[r // NPASS]
+            if pw == 0:
+                return
+            ip = ipp.tile([P, 1024], BF16, name="ip", tag="ip")
+            ips[r] = ip
+            for h0 in range(0, pw, P):
+                nc.tensor.matmul(
+                    out=ip[:, 4 * h0 : 4 * h0 + 512],
+                    lhsT=identb[:],
+                    rhs=raws[r][:, :, HW - pw + h0 : HW - pw + h0 + P].rearrange("p t c -> p c t"),
+                    start=True,
+                    stop=True,
+                )
+
+        def pe_copy(r):
+            pw = PW[r // NPASS]
+            if r in gw:
+                return
             gr = grp.tile([P, HW, 4], BF16, name="gr", tag="gr", align_bytes=64)
             grouped[r] = gr
+            if pw == 0:
+                return
+            nc.scalar.copy(
+                out=gr[:, HW - pw : HW, :].rearrange("p c t -> p (c t)").bitcast(F32),
+                in_=ips[r][:, 0 : 4 * pw].bitcast(F32),
+            )
+
+        def direct_g(r):
+            gr = ggp.tile([P, HW, 4], BF16, name="gg", tag="gg", align_bytes=64)
+            grouped[r] = gr
+            if gw[r] > 0:
+                nc.gpsimd.tensor_scalar(
+                    out=gr[:, HW - gw[r] : HW, :],
+                    in0=raws[r][:, :, HW - gw[r] : HW].rearrange("p t w -> p w t"),
+                    scalar1=1.0,
+                    scalar2=0.0,
+                    op0=ALU.mult,
+                    op1=ALU.add,
+                )
+
+        def direct_v(r):
+            wa = min(WA[r // NPASS], HW - gw.get(r, 0))
             if wa > 0:
                 nc.vector.tensor_copy(
-                    out=gr[:, 0:wa, :].rearrange("p (c i) t -> p c t i", i=4),
-                    in_=raw[:, :, 0:wa].rearrange("p t (c i) -> p c t i", i=4),
+                    out=grouped[r][:, 0:wa, :].rearrange("p (c i) t -> p c t i", i=4),
+                    in_=raws[r][:, :, 0:wa].rearrange("p t (c i) -> p c t i", i=4),
                 )
-            if wa < HW:
+
+        def direct_s(r):
+            wa = min(WA[r // NPASS], HW - gw.get(r, 0))
+            sw = HW - (gw[r] if r in gw else PW[r // NPASS])
+            if wa < sw:
                 nc.scalar.copy(
-                    out=gr[:, wa:HW, :].rearrange("p (c i) t -> p c t i", i=4),
-                    in_=raw[:, :, wa:HW].rearrange("p t (c i) -> p c t i", i=4),
+                    out=grouped[r][:, wa:sw, :].rearrange("p (c i) t -> p c t i", i=4),
+                    in_=raws[r][:, :, wa:sw].rearrange("p t (c i) -> p c t i", i=4),
                 )
 
         def quant(r):
@@ -101,24 +160,30 @@ def tile_slstmcell_kernel(tc, x_t, h_prev, c_prev, n_prev, W, R, b, out_0, out_1
                 in_=grouped[r][:].rearrange("p w t -> p (w t)"),
             )
 
-        def x_prep(c):
+        xts = {}
+        gxs = {}
+
+        def x_turn(k):
+            c, pair = k // 2, k % 2
             s, half = c // 2, c % 2
-            gx = gxp.tile([P, B, 4], BF16, name="gx", tag="gx", align_bytes=64)
-            gx_w = gx[:].bitcast(F32)
-            for pair in range(2):
-                xt = tpp.tile([P, 2, 256], F32, name="xt", tag="tp")
-                for bl in range(2):
-                    bt = 2 * pair + bl
-                    words = xh_w[:, s, bt, 256 * half : 256 * half + 256].rearrange("p (q u) -> p q u", u=2)
-                    for u in range(2):
-                        nc.tensor.transpose(
-                            out=xt[:, u, bl * P : (bl + 1) * P], in_=words[:, :, u], identity=ident[:]
-                        )
-                nc.scalar.copy(
-                    out=gx_w[:, 256 * pair : 256 * pair + 256, :], in_=xt[:].rearrange("q u n -> q n u")
-                )
+            xt = (accp if k < 4 else tpp).tile([P, 2, 256], F32, name="xt", tag=("acc" if k < 4 else "tp"))
+            xts[k] = xt
+            for bl in range(2):
+                bt = 2 * pair + bl
+                words = xh_w[:, s, bt, 256 * half : 256 * half + 256].rearrange("p (q u) -> p q u", u=2)
+                for u in range(2):
+                    nc.tensor.transpose(out=xt[:, u, bl * P : (bl + 1) * P], in_=words[:, :, u], identity=ident[:])
+
+        def x_copy(k):
+            c, pair = k // 2, k % 2
+            if pair == 0:
+                gxs[c] = gxp.tile([P, B, 4], BF16, name="gx", tag="gx", align_bytes=64)
+            gx_w = gxs[c][:].bitcast(F32)
+            nc.scalar.copy(out=gx_w[:, 256 * pair : 256 * pair + 256, :], in_=xts[k][:].rearrange("q u n -> q n u"))
+
+        def x_quant(c):
             nc.vector.quantize_mx(
-                out=xq[:, c, :].bitcast(FP8X4), scales=xs[:, c, :], in_=gx[:].rearrange("p n t -> p (n t)")
+                out=xq[:, c, :].bitcast(FP8X4), scales=xs[:, c, :], in_=gxs[c][:].rearrange("p n t -> p (n t)")
             )
 
         def bias_prep():
@@ -133,38 +198,23 @@ def tile_slstmcell_kernel(tc, x_t, h_prev, c_prev, n_prev, W, R, b, out_0, out_1
 
         accs = {}
 
-        def mm_pass(t, c):
-            q, jl = t // 4, t % 4
-            if c == 0:
-                accs[t] = accp.tile([P, B], F32, name="acc", tag="acc")
-            nc.tensor.matmul_mx(
-                out=accs[t][:],
-                lhsT=wq[q][:, c, jl * P : (jl + 1) * P].bitcast(FP8X4),
-                lhsT_scale=ws[q][:, c, jl * P : (jl + 1) * P],
-                rhs=xq[:, c, :].bitcast(FP8X4),
-                rhs_scale=xs[:, c, :],
-                start=(c == 0),
-                stop=(c == NPASS - 1),
-            )
+        def passes(r):
+            q, c = r // NPASS, r % NPASS
+            for jl in range(4):
+                t = 4 * q + jl
+                if c == 0:
+                    accs[t] = accp.tile([P, B], F32, name="acc", tag="acc")
+                nc.tensor.matmul_mx(
+                    out=accs[t][:],
+                    lhsT=wq[q][:, c, jl * P : (jl + 1) * P].bitcast(FP8X4),
+                    lhsT_scale=ws[q][:, c, jl * P : (jl + 1) * P],
+                    rhs=xq[:, c, :].bitcast(FP8X4),
+                    rhs_scale=xs[:, c, :],
+                    start=(c == 0),
+                    stop=(c == NPASS - 1),
+                )
 
         FUNC = {GZ: ACT.Tanh, GI: ACT.Exp, GF: ACT.Sigmoid, GO: ACT.Tanh}
-
-        def gate_act(t, out_ap):
-            g, j = ORDER[t // 8], t % 8
-            col = g * 8 + j
-            nc.scalar.activation(
-                out=out_ap,
-                in_=accs[t][:],
-                func=FUNC[g],
-                bias=bias_sb[:, col : col + 1],
-                scale=(0.5 if g == GO else 1.0),
-            )
-
-        def back(src_ap):
-            ps = tpp.tile([P, BT, P], F32, name="ps", tag="tp")
-            for bt in range(BT):
-                nc.tensor.transpose(out=ps[:, bt, :], in_=src_ap[:, bt * P : (bt + 1) * P], identity=ident[:])
-            return ps
 
         o_h = out_0.rearrange("(p t) h -> p t h", t=BT)
         o_c = out_1.rearrange("(p t) h -> p t h", t=BT)
@@ -191,111 +241,158 @@ def tile_slstmcell_kernel(tc, x_t, h_prev, c_prev, n_prev, W, R, b, out_0, out_1
         nn = big.tile([P, BT, H], F32, name="nn", tag="big")
         eT = big.tile([P, 8, B], F32, name="eT", tag="big")
         late = {}
-
         gts = {}
-        state = {"next_load": RAW_BUFS}
+        gTs = {}
+        pss = {}
 
-        def rq(q):
-            for c in range(NPASS + 1):
-                r = NPASS * q + c
-                if c < NPASS:
-                    regroup(r)
-                    if state["next_load"] < 32:
-                        load_unit(state["next_load"])
-                        state["next_load"] += 1
-                if c > 0:
-                    quant(r - 1)
-                    if q == 0:
-                        x_prep(c - 1)
-                    for t in range(4 * q, 4 * q + 4):
-                        mm_pass(t, c - 1)
-
-        def front(q):
-            g, half = ORDER[q // 2], q % 2
+        def acts(q):
+            g = ORDER[q // 2]
             if g != GI:
-                gT = gtp.tile([P, 4, B], F32, name="gT", tag="gT")
+                gTs[q] = gtp.tile([P, 4, B], F32, name="gT", tag="gT")
             for t in range(4 * q, 4 * q + 4):
-                if g == GI:
-                    gts[t] = eT[:, t % 8, :]
-                else:
-                    gts[t] = gT[:, t % 4, :]
-                gate_act(t, gts[t])
-            if g == GZ:
-                nc.vector.scalar_tensor_tensor(
-                    out=gT[:], in0=eT[:, 4 * half : 4 * half + 4, :], scalar=50.0, in1=gT[:], op0=ALU.min, op1=ALU.mult
-                )
-
-        def recip():
-            late["sq"] = big.tile([P, BT, H], F32, name="sq", tag="big")
-            late["sg"] = big.tile([P, BT, H], F32, name="sg", tag="big")
-            sq, sg = late["sq"], late["sg"]
-            for h in range(2):
+                gts[t] = eT[:, t % 8, :] if g == GI else gTs[q][:, t % 4, :]
+                col = g * 8 + t % 8
                 nc.scalar.activation(
-                    out=sq[:, :, halfcols(h)],
-                    in_=nn[:, :, halfcols(h)],
-                    func=ACT.Abs_reciprocal_sqrt,
-                    bias=EPS,
-                    scale=1.0,
+                    out=gts[t],
+                    in_=accs[t][:],
+                    func=FUNC[g],
+                    bias=bias_sb[:, col : col + 1],
+                    scale=(0.5 if g == GO else 1.0),
                 )
-            for h in range(2):
-                nc.vector.tensor_scalar(
-                    out=sg[:, :, halfcols(h)],
-                    in0=nn[:, :, halfcols(h)],
-                    scalar1=-EPS,
-                    scalar2=0.5,
-                    op0=ALU.is_ge,
-                    op1=ALU.subtract,
-                )
-                nc.scalar.activation(out=sq[:, :, halfcols(h)], in_=sq[:, :, halfcols(h)], func=ACT.Square)
-            for h in range(2):
-                nc.vector.tensor_tensor(
-                    out=sq[:, :, halfcols(h)], in0=sq[:, :, halfcols(h)], in1=sg[:, :, halfcols(h)], op=ALU.mult
-                )
-            late["hh"] = big.tile([P, BT, H], F32, name="hh", tag="big")
 
-        def rear(q):
+        def zmul(q):
+            half = q % 2
+            nc.vector.scalar_tensor_tensor(
+                out=gTs[q][:], in0=eT[:, 4 * half : 4 * half + 4, :], scalar=50.0, in1=gTs[q][:], op0=ALU.min, op1=ALU.mult
+            )
+
+        def back(t):
+            ps = tpp.tile([P, BT, P], F32, name="ps", tag="tp")
+            for bt in range(BT):
+                nc.tensor.transpose(out=ps[:, bt, :], in_=gts[t][:, bt * P : (bt + 1) * P], identity=ident[:])
+            pss[t] = ps
+
+        def rear_tile(t):
+            g, j = ORDER[t // 8], t % 8
+            js = cols(j)
+            ps = pss[t]
+            if g == GF:
+                nc.vector.tensor_tensor(out=cc[:, :, js], in0=ps[:], in1=cprev[:, :, js], op=ALU.mult)
+                nc.vector.tensor_tensor(out=nn[:, :, js], in0=ps[:], in1=nprev[:, :, js], op=ALU.mult)
+            elif g == GI:
+                nc.vector.scalar_tensor_tensor(
+                    out=nn[:, :, js], in0=ps[:], scalar=50.0, in1=nn[:, :, js], op0=ALU.min, op1=ALU.add
+                )
+            elif g == GZ:
+                nc.vector.tensor_tensor(out=cc[:, :, js], in0=ps[:], in1=cc[:, :, js], op=ALU.add)
+            else:
+                hh = late["hh"]
+                nc.vector.scalar_tensor_tensor(
+                    out=hh[:, :, js], in0=ps[:], scalar=1.0, in1=hh[:, :, js], op0=ALU.add, op1=ALU.mult
+                )
+                if j >= 6:
+                    nc.sync.dma_start(out=o_h[:, :, js], in_=hh[:, :, js])
+                elif j % 2 == 1:
+                    hs = slice((j - 1) * P, (j + 1) * P)
+                    nc.sync.dma_start(out=o_h[:, :, hs], in_=hh[:, :, hs])
+
+        def rear_block(q):
             g, half = ORDER[q // 2], q % 2
-            for t in range(4 * q, 4 * q + 4):
-                j = t % 8
-                js = cols(j)
-                ps = back(gts[t])
-                if g == GF:
-                    nc.vector.tensor_tensor(out=cc[:, :, js], in0=ps[:], in1=cprev[:, :, js], op=ALU.mult)
-                    nc.vector.tensor_tensor(out=nn[:, :, js], in0=ps[:], in1=nprev[:, :, js], op=ALU.mult)
-                elif g == GI:
-                    nc.vector.scalar_tensor_tensor(
-                        out=nn[:, :, js], in0=ps[:], scalar=50.0, in1=nn[:, :, js], op0=ALU.min, op1=ALU.add
-                    )
-                elif g == GZ:
-                    nc.vector.tensor_tensor(out=cc[:, :, js], in0=ps[:], in1=cc[:, :, js], op=ALU.add)
-                else:
-                    nc.vector.scalar_tensor_tensor(
-                        out=late["hh"][:, :, js], in0=ps[:], scalar=1.0, in1=late["hh"][:, :, js], op0=ALU.add, op1=ALU.mult
-                    )
-                    if j >= 6:
-                        nc.sync.dma_start(out=o_h[:, :, js], in_=late["hh"][:, :, js])
-                    elif j % 2 == 1:
-                        hs = slice((j - 1) * P, (j + 1) * P)
-                        nc.sync.dma_start(out=o_h[:, :, hs], in_=late["hh"][:, :, hs])
+            t0 = 4 * q
+            for j in range(4):
+                rear_tile(t0 + j)
+                if j + TPB < 4:
+                    back(t0 + j + TPB)
             hs = halfcols(half)
             if g == GI:
                 nc.sync.dma_start(out=o_n[:, :, hs], in_=nn[:, :, hs])
-                if half == 1:
-                    recip()
             if g == GZ:
                 nc.sync.dma_start(out=o_c[:, :, hs], in_=cc[:, :, hs])
-                nc.vector.tensor_tensor(
-                    out=late["hh"][:, :, hs], in0=cc[:, :, hs], in1=late["sq"][:, :, hs], op=ALU.mult
-                )
 
-        for q in range(5):
-            rq(q)
-            if q == 0:
-                bias_prep()
-            front(q)
-            rear(q)
-        for q in range(5, 8):
-            rq(q)
-            front(q)
-        for q in range(5, 8):
-            rear(q)
+        def ars(h):
+            if h == 0:
+                late["sq"] = big.tile([P, BT, H], F32, name="sq", tag="big")
+            nc.scalar.activation(
+                out=late["sq"][:, :, halfcols(h)], in_=nn[:, :, halfcols(h)], func=ACT.Abs_reciprocal_sqrt, bias=EPS, scale=1.0
+            )
+
+        def sign(h):
+            if h == 0:
+                late["sg"] = big.tile([P, BT, H], F32, name="sg", tag="big")
+            nc.vector.tensor_scalar(
+                out=late["sg"][:, :, halfcols(h)], in0=nn[:, :, halfcols(h)], scalar1=-EPS, scalar2=0.5, op0=ALU.is_ge, op1=ALU.subtract
+            )
+
+        def square(h):
+            sq = late["sq"]
+            nc.scalar.activation(out=sq[:, :, halfcols(h)], in_=sq[:, :, halfcols(h)], func=ACT.Square)
+
+        def signed(h):
+            sq, sg = late["sq"], late["sg"]
+            nc.vector.tensor_tensor(out=sq[:, :, halfcols(h)], in0=sq[:, :, halfcols(h)], in1=sg[:, :, halfcols(h)], op=ALU.mult)
+
+        def cdiv(h):
+            if h == 0:
+                late["hh"] = big.tile([P, BT, H], F32, name="hh", tag="big")
+            nc.vector.tensor_tensor(
+                out=late["hh"][:, :, halfcols(h)], in0=cc[:, :, halfcols(h)], in1=late["sq"][:, :, halfcols(h)], op=ALU.mult
+            )
+
+        plan = {}
+
+        def at(step, phase, fn, *args):
+            plan.setdefault(step, []).append((phase, len(plan.get(step, ())), fn, args))
+
+        def pass_step(u):
+            return max(u + (LP if u < NU - LP0 else 0), XS + 1 + min(u, 3))
+
+        def rear_step(q):
+            return pass_step(4 * q + 3) + 2 + (1 if ORDER[q // 2] == GZ else 0)
+
+        chain = [rear_step(q) for q in range(6)] + [NU - 1]
+        for k, u in enumerate(chain):
+            gw[u] = 0 if k == 0 else (GWF if ORDER[(k - 1) // 2] == GF else GWO)
+            at(chain[k - 1] if k > 0 else u - LC, 6.5 if k > 0 else 1, direct_g, u)
+
+        for u in range(NU):
+            at(u - LI, 0, pe_ident, u)
+            at(u - LC, 1, pe_copy, u)
+            at(u - LDS, 3, direct_s, u)
+            at(u - 1, 4, direct_v, u)
+            if u + RAW_BUFS < NU:
+                at(u - 1, 5, load_unit, u + RAW_BUFS)
+            at(u, 6, quant, u)
+            at(pass_step(u), 12, passes, u)
+        for k in range(4):
+            at(XS + k, 0, x_turn, 2 * k)
+            at(XS + k, 0, x_turn, 2 * k + 1)
+            at(XS + k, 2, x_copy, 2 * k)
+            at(XS + k, 2, x_copy, 2 * k + 1)
+            at(XS + k + 1, 8, x_quant, k)
+        at(XS + 2, 8.5, bias_prep)
+        for q in range(8):
+            g = ORDER[q // 2]
+            e = pass_step(4 * q + 3)
+            z = 1 if g == GZ else 0
+            at(e + 1, 2, acts, q)
+            if z:
+                at(e + 1, 9, zmul, q)
+            for j in range(TPB):
+                at(e + 1 + z, 10, back, 4 * q + j)
+            at(e + 2 + z if q < 6 else NU + 1, 7 + 0.01 * q, rear_block, q)
+            if z:
+                at(e + 4, 9, cdiv, q % 2)
+        e3 = pass_step(15) + 2
+        at(e3 + 1, 2, ars, 0)
+        at(e3 + 1, 2, ars, 1)
+        at(e3 + SQ, 2.5, square, 0)
+        at(e3 + SQ + 1, 2.5, square, 1)
+        at(e3 + 1, 9, sign, 0)
+        at(e3 + 2, 9, sign, 1)
+        at(e3 + SQ + 1, 8.9, signed, 0)
+        at(e3 + SQ + 2, 8.9, signed, 1)
+
+        ctx.enter_context(tc.manual_schedule(engines={ENG.PE, ENG.DVE, ENG.Activation, ENG.Pool}))
+        for step in sorted(plan):
+            for phase, k, fn, args in sorted(plan[step], key=lambda it: (it[0], it[1])):
+                fn(*args)

@@ -25,16 +25,30 @@ EPS = 1e-6
 FLOPS = 2 * 512 * 2048 * 4096
 
 WA = (256, 256, 32, 192, 352, 512, 0, 64)
-PW = (0, 0, 0, 0, 0, 0, 0, 0)
+GW_TWO_READS, GW_ONE_READ = 512, 288
 RAW_BUFS = 8
-LI, LC, LDS = 3, 2, 2
-LP = 1
-XS = 1
-TPB = 4
-GRB = 6
-SQ = 3
-LP0 = 8
-GWF, GWO = 512, 288
+LEAD_SCALAR = 2
+LAG_PASSES = 1
+PROMPT_UNITS = 8
+X_STEP = 1
+LAG_SQUARE = 3
+
+PH_TURN_X = 0
+PH_NEW_TILE = 1
+PH_SCALAR_FIRST = 2
+PH_SQUARE = 3
+PH_SCALAR_COPY = 4
+PH_VECTOR_COPY = 5
+PH_LOAD = 6
+PH_QUANT = 7
+PH_GPSIMD = 8
+PH_REAR = 9
+PH_QUANT_X = 10
+PH_BIAS = 11
+PH_SIGNED = 12
+PH_VECTOR_LAST = 13
+PH_BACK = 14
+PH_PASSES = 15
 
 
 def tile_slstmcell_kernel(tc, x_t, h_prev, c_prev, n_prev, W, R, b, out_0, out_1, out_2):
@@ -44,18 +58,15 @@ def tile_slstmcell_kernel(tc, x_t, h_prev, c_prev, n_prev, W, R, b, out_0, out_1
         big = ctx.enter_context(tc.tile_pool(name="big", bufs=5))
         gxp = ctx.enter_context(tc.tile_pool(name="gxp", bufs=2))
         rawp = ctx.enter_context(tc.tile_pool(name="rawp", bufs=RAW_BUFS))
-        grp = ctx.enter_context(tc.tile_pool(name="grp", bufs=GRB))
+        grp = ctx.enter_context(tc.tile_pool(name="grp", bufs=6))
         ggp = ctx.enter_context(tc.tile_pool(name="ggp", bufs=1))
         wqp = ctx.enter_context(tc.tile_pool(name="wqp", bufs=3))
         gtp = ctx.enter_context(tc.tile_pool(name="gtp", bufs=3))
         accp = ctx.enter_context(tc.psum_pool(name="accp", bufs=4))
-        tpp = ctx.enter_context(tc.psum_pool(name="tpp", bufs=TPB))
-        ipp = ctx.enter_context(tc.psum_pool(name="ipp", bufs=4 - TPB)) if TPB < 4 else None
+        tpp = ctx.enter_context(tc.psum_pool(name="tpp", bufs=4))
 
         ident = const.tile([P, P], F32, name="ident")
         make_identity(nc, ident[:])
-        identb = const.tile([P, P], BF16, name="identb")
-        make_identity(nc, identb[:])
         braw = const.tile([P, P], BF16, name="braw")
         nc.vector.memset(braw[:], 0.0)
         nc.scalar.dma_start(out=braw[0:32, :], in_=b.rearrange("(r c) -> r c", c=P))
@@ -75,12 +86,11 @@ def tile_slstmcell_kernel(tc, x_t, h_prev, c_prev, n_prev, W, R, b, out_0, out_1
         raws = {}
         gw = {}
         grouped = {}
-        ips = {}
         wq = {}
         ws = {}
 
-        def load_unit(r):
-            q, c = r // NPASS, r % NPASS
+        def load_unit(u):
+            q, c = u // NPASS, u % NPASS
             g, half = ORDER[q // 2], q % 2
             src = W if c < 2 else R
             r0 = 512 * (c % 2)
@@ -89,75 +99,54 @@ def tile_slstmcell_kernel(tc, x_t, h_prev, c_prev, n_prev, W, R, b, out_0, out_1
             nc.sync.dma_start(
                 out=raw[:], in_=src[r0 : r0 + 512, c0 : c0 + HW].rearrange("(p j) w -> p j w", j=4)
             )
-            raws[r] = raw
+            raws[u] = raw
 
-        def pe_ident(r):
-            pw = PW[r // NPASS]
-            if pw == 0:
-                return
-            ip = ipp.tile([P, 1024], BF16, name="ip", tag="ip")
-            ips[r] = ip
-            for h0 in range(0, pw, P):
-                nc.tensor.matmul(
-                    out=ip[:, 4 * h0 : 4 * h0 + 512],
-                    lhsT=identb[:],
-                    rhs=raws[r][:, :, HW - pw + h0 : HW - pw + h0 + P].rearrange("p t c -> p c t"),
-                    start=True,
-                    stop=True,
-                )
+        def new_tile(u):
+            if u not in gw:
+                grouped[u] = grp.tile([P, HW, 4], BF16, name="gr", tag="gr", align_bytes=64)
 
-        def pe_copy(r):
-            pw = PW[r // NPASS]
-            if r in gw:
-                return
-            gr = grp.tile([P, HW, 4], BF16, name="gr", tag="gr", align_bytes=64)
-            grouped[r] = gr
-            if pw == 0:
-                return
-            nc.scalar.copy(
-                out=gr[:, HW - pw : HW, :].rearrange("p c t -> p (c t)").bitcast(F32),
-                in_=ips[r][:, 0 : 4 * pw].bitcast(F32),
-            )
-
-        def direct_g(r):
+        def gpsimd_copy(u):
             gr = ggp.tile([P, HW, 4], BF16, name="gg", tag="gg", align_bytes=64)
-            grouped[r] = gr
-            if gw[r] > 0:
+            grouped[u] = gr
+            if gw[u] > 0:
                 nc.gpsimd.tensor_scalar(
-                    out=gr[:, HW - gw[r] : HW, :],
-                    in0=raws[r][:, :, HW - gw[r] : HW].rearrange("p t w -> p w t"),
+                    out=gr[:, HW - gw[u] : HW, :],
+                    in0=raws[u][:, :, HW - gw[u] : HW].rearrange("p t w -> p w t"),
                     scalar1=1.0,
                     scalar2=0.0,
                     op0=ALU.mult,
                     op1=ALU.add,
                 )
 
-        def direct_v(r):
-            wa = min(WA[r // NPASS], HW - gw.get(r, 0))
+        def vector_cols(u):
+            return min(WA[u // NPASS], HW - gw.get(u, 0))
+
+        def vector_copy(u):
+            wa = vector_cols(u)
             if wa > 0:
                 nc.vector.tensor_copy(
-                    out=grouped[r][:, 0:wa, :].rearrange("p (c i) t -> p c t i", i=4),
-                    in_=raws[r][:, :, 0:wa].rearrange("p t (c i) -> p c t i", i=4),
+                    out=grouped[u][:, 0:wa, :].rearrange("p (c i) t -> p c t i", i=4),
+                    in_=raws[u][:, :, 0:wa].rearrange("p t (c i) -> p c t i", i=4),
                 )
 
-        def direct_s(r):
-            wa = min(WA[r // NPASS], HW - gw.get(r, 0))
-            sw = HW - (gw[r] if r in gw else PW[r // NPASS])
+        def scalar_copy(u):
+            wa = vector_cols(u)
+            sw = HW - gw.get(u, 0)
             if wa < sw:
                 nc.scalar.copy(
-                    out=grouped[r][:, wa:sw, :].rearrange("p (c i) t -> p c t i", i=4),
-                    in_=raws[r][:, :, wa:sw].rearrange("p t (c i) -> p c t i", i=4),
+                    out=grouped[u][:, wa:sw, :].rearrange("p (c i) t -> p c t i", i=4),
+                    in_=raws[u][:, :, wa:sw].rearrange("p t (c i) -> p c t i", i=4),
                 )
 
-        def quant(r):
-            q, c = r // NPASS, r % NPASS
+        def quant(u):
+            q, c = u // NPASS, u % NPASS
             if c == 0:
                 wq[q] = wqp.tile([P, NPASS, HW], U32, name="wq", tag="wq", align_bytes=64)
                 ws[q] = wqp.tile([P, NPASS, HW], U8, name="ws", tag="ws", align_bytes=64)
             nc.vector.quantize_mx(
                 out=wq[q][:, c, :].bitcast(FP8X4),
                 scales=ws[q][:, c, :],
-                in_=grouped[r][:].rearrange("p w t -> p (w t)"),
+                in_=grouped[u][:].rearrange("p w t -> p (w t)"),
             )
 
         xts = {}
@@ -198,8 +187,8 @@ def tile_slstmcell_kernel(tc, x_t, h_prev, c_prev, n_prev, W, R, b, out_0, out_1
 
         accs = {}
 
-        def passes(r):
-            q, c = r // NPASS, r % NPASS
+        def passes(u):
+            q, c = u // NPASS, u % NPASS
             for jl in range(4):
                 t = 4 * q + jl
                 if c == 0:
@@ -232,8 +221,8 @@ def tile_slstmcell_kernel(tc, x_t, h_prev, c_prev, n_prev, W, R, b, out_0, out_1
         load_unit(2)
         load_unit(3)
         nc.sync.dma_start(out=xh[:, 1], in_=h_prev.rearrange("(p t) k -> p t k", t=BT))
-        for r in range(4, RAW_BUFS):
-            load_unit(r)
+        for u in range(4, RAW_BUFS):
+            load_unit(u)
         nc.sync.dma_start(out=cprev[:], in_=c_prev.rearrange("(p t) h -> p t h", t=BT))
         nc.sync.dma_start(out=nprev[:], in_=n_prev.rearrange("(p t) h -> p t h", t=BT))
 
@@ -298,11 +287,8 @@ def tile_slstmcell_kernel(tc, x_t, h_prev, c_prev, n_prev, W, R, b, out_0, out_1
 
         def rear_block(q):
             g, half = ORDER[q // 2], q % 2
-            t0 = 4 * q
-            for j in range(4):
-                rear_tile(t0 + j)
-                if j + TPB < 4:
-                    back(t0 + j + TPB)
+            for t in range(4 * q, 4 * q + 4):
+                rear_tile(t)
             hs = halfcols(half)
             if g == GI:
                 nc.sync.dma_start(out=o_n[:, :, hs], in_=nn[:, :, hs])
@@ -344,53 +330,53 @@ def tile_slstmcell_kernel(tc, x_t, h_prev, c_prev, n_prev, W, R, b, out_0, out_1
             plan.setdefault(step, []).append((phase, len(plan.get(step, ())), fn, args))
 
         def pass_step(u):
-            return max(u + (LP if u < NU - LP0 else 0), XS + 1 + min(u, 3))
+            return max(u + (LAG_PASSES if u < NU - PROMPT_UNITS else 0), X_STEP + 1 + min(u, 3))
 
         def rear_step(q):
             return pass_step(4 * q + 3) + 2 + (1 if ORDER[q // 2] == GZ else 0)
 
         chain = [rear_step(q) for q in range(6)] + [NU - 1]
         for k, u in enumerate(chain):
-            gw[u] = 0 if k == 0 else (GWF if ORDER[(k - 1) // 2] == GF else GWO)
-            at(chain[k - 1] if k > 0 else u - LC, 6.5 if k > 0 else 1, direct_g, u)
+            if k == 0:
+                gw[u] = 0
+                at(u - LEAD_SCALAR, PH_NEW_TILE, gpsimd_copy, u)
+            else:
+                gw[u] = GW_TWO_READS if ORDER[(k - 1) // 2] == GF else GW_ONE_READ
+                at(chain[k - 1], PH_GPSIMD, gpsimd_copy, u)
 
         for u in range(NU):
-            at(u - LI, 0, pe_ident, u)
-            at(u - LC, 1, pe_copy, u)
-            at(u - LDS, 3, direct_s, u)
-            at(u - 1, 4, direct_v, u)
+            at(u - LEAD_SCALAR, PH_NEW_TILE, new_tile, u)
+            at(u - LEAD_SCALAR, PH_SCALAR_COPY, scalar_copy, u)
+            at(u - 1, PH_VECTOR_COPY, vector_copy, u)
             if u + RAW_BUFS < NU:
-                at(u - 1, 5, load_unit, u + RAW_BUFS)
-            at(u, 6, quant, u)
-            at(pass_step(u), 12, passes, u)
-        for k in range(4):
-            at(XS + k, 0, x_turn, 2 * k)
-            at(XS + k, 0, x_turn, 2 * k + 1)
-            at(XS + k, 2, x_copy, 2 * k)
-            at(XS + k, 2, x_copy, 2 * k + 1)
-            at(XS + k + 1, 8, x_quant, k)
-        at(XS + 2, 8.5, bias_prep)
+                at(u - 1, PH_LOAD, load_unit, u + RAW_BUFS)
+            at(u, PH_QUANT, quant, u)
+            at(pass_step(u), PH_PASSES, passes, u)
+        for c in range(NPASS):
+            at(X_STEP + c, PH_TURN_X, x_turn, 2 * c)
+            at(X_STEP + c, PH_TURN_X, x_turn, 2 * c + 1)
+            at(X_STEP + c, PH_SCALAR_FIRST, x_copy, 2 * c)
+            at(X_STEP + c, PH_SCALAR_FIRST, x_copy, 2 * c + 1)
+            at(X_STEP + c + 1, PH_QUANT_X, x_quant, c)
+        at(X_STEP + 2, PH_BIAS, bias_prep)
         for q in range(8):
-            g = ORDER[q // 2]
-            e = pass_step(4 * q + 3)
-            z = 1 if g == GZ else 0
-            at(e + 1, 2, acts, q)
-            if z:
-                at(e + 1, 9, zmul, q)
-            for j in range(TPB):
-                at(e + 1 + z, 10, back, 4 * q + j)
-            at(e + 2 + z if q < 6 else NU + 1, 7 + 0.01 * q, rear_block, q)
-            if z:
-                at(e + 4, 9, cdiv, q % 2)
-        e3 = pass_step(15) + 2
-        at(e3 + 1, 2, ars, 0)
-        at(e3 + 1, 2, ars, 1)
-        at(e3 + SQ, 2.5, square, 0)
-        at(e3 + SQ + 1, 2.5, square, 1)
-        at(e3 + 1, 9, sign, 0)
-        at(e3 + 2, 9, sign, 1)
-        at(e3 + SQ + 1, 8.9, signed, 0)
-        at(e3 + SQ + 2, 8.9, signed, 1)
+            is_z = ORDER[q // 2] == GZ
+            a = pass_step(4 * q + 3) + 1
+            at(a, PH_SCALAR_FIRST, acts, q)
+            if is_z:
+                at(a, PH_VECTOR_LAST, zmul, q)
+            for j in range(4):
+                at(rear_step(q) - 1, PH_BACK, back, 4 * q + j)
+            at(rear_step(q) if q < 6 else NU + 1, PH_REAR, rear_block, q)
+            if is_z:
+                at(a + 3, PH_VECTOR_LAST, cdiv, q % 2)
+        n_done = rear_step(3)
+        at(n_done + 1, PH_SCALAR_FIRST, ars, 0)
+        at(n_done + 1, PH_SCALAR_FIRST, ars, 1)
+        for h in range(2):
+            at(n_done + LAG_SQUARE + h, PH_SQUARE, square, h)
+            at(n_done + 1 + h, PH_VECTOR_LAST, sign, h)
+            at(n_done + LAG_SQUARE + 1 + h, PH_SIGNED, signed, h)
 
         ctx.enter_context(tc.manual_schedule(engines={ENG.PE, ENG.DVE, ENG.Activation, ENG.Pool}))
         for step in sorted(plan):

@@ -24,20 +24,43 @@ ORDER = (GF, GI, GZ, GO)
 EPS = 1e-6
 FLOPS = 2 * 512 * 2048 * 4096
 
-WA = (256, 256, 32, 192, 352, 512, 0, 64)
-GW_TWO_READS, GW_ONE_READ = 512, 288
-RAW_BUFS = 8
+WA = (256, 256, 32, 64, 352, 512, 0, 64)
+PE_COLS = 256
+ID_AT = 0
+EV_AT = 1
+ID_TO = 2
+ID_N = (0,)*8
+EV_PER = 2
+ST_UNITS = ()
+ST_COLS = 256
+ST_LEAD = 2
+BIAS_AT = -3
+N_FIRST = False
 LEAD_SCALAR = 2
+LEAD_GEV = 2
+LAG_ACT = (0, 3, 0, 1, 1, 1, 0, 0)
+LAG_REAR = (0, 0, 0, 0, 0, 0, 0, 0)
 LAG_PASSES = 1
 PROMPT_UNITS = 8
-X_STEP = 1
+BUB = 3
+RAW_BUFS = 4
+GR_BUFS = 6
+GG_BUFS = 3
+FIRST_CUTS = (1, 1, 1, 1)
+FIRST_LOADS = ("f0", "x", "f1", "h", "f2", "f3", "n", "c")
+X_STEPS = (0, 1, 2, 3)
 LAG_SQUARE = 3
+LAG_ARS = 1
+LAG_CDIV = 3
+GW = ((352,352), (352,352), (288,), (288,), (288,), (288,))
+G_OFF = 3
 
 PH_TURN_X = 0
 PH_NEW_TILE = 1
 PH_SCALAR_FIRST = 2
 PH_SQUARE = 3
 PH_SCALAR_COPY = 4
+PH_HALVE = 4.5
 PH_VECTOR_COPY = 5
 PH_LOAD = 6
 PH_QUANT = 7
@@ -48,6 +71,8 @@ PH_BIAS = 11
 PH_SIGNED = 12
 PH_VECTOR_LAST = 13
 PH_BACK = 14
+PH_IDENT = 15.5
+PH_ONE = 8.5
 PH_PASSES = 15
 
 
@@ -58,8 +83,9 @@ def tile_slstmcell_kernel(tc, x_t, h_prev, c_prev, n_prev, W, R, b, out_0, out_1
         big = ctx.enter_context(tc.tile_pool(name="big", bufs=5))
         gxp = ctx.enter_context(tc.tile_pool(name="gxp", bufs=2))
         rawp = ctx.enter_context(tc.tile_pool(name="rawp", bufs=RAW_BUFS))
-        grp = ctx.enter_context(tc.tile_pool(name="grp", bufs=6))
-        ggp = ctx.enter_context(tc.tile_pool(name="ggp", bufs=1))
+        grp = ctx.enter_context(tc.tile_pool(name="grp", bufs=GR_BUFS))
+        ggp = ctx.enter_context(tc.tile_pool(name="ggp", bufs=GG_BUFS))
+        onep = ctx.enter_context(tc.tile_pool(name="onep", bufs=2))
         wqp = ctx.enter_context(tc.tile_pool(name="wqp", bufs=3))
         gtp = ctx.enter_context(tc.tile_pool(name="gtp", bufs=3))
         accp = ctx.enter_context(tc.psum_pool(name="accp", bufs=4))
@@ -67,13 +93,16 @@ def tile_slstmcell_kernel(tc, x_t, h_prev, c_prev, n_prev, W, R, b, out_0, out_1
 
         ident = const.tile([P, P], F32, name="ident")
         make_identity(nc, ident[:])
+        identb = const.tile([P, P], BF16, name="identb")
+        make_identity(nc, identb[:])
         braw = const.tile([P, P], BF16, name="braw")
-        nc.vector.memset(braw[:], 0.0)
         nc.scalar.dma_start(out=braw[0:32, :], in_=b.rearrange("(r c) -> r c", c=P))
+        nc.vector.memset(braw[32:64, :], 0.0)
+        nc.vector.memset(braw[64:128, :], 0.0)
         bias_sb = const.tile([P, 32], F32, name="bias_sb")
         warm = const.tile([P, 1], F32, name="warm")
         nc.vector.memset(warm[:], 0.0)
-        nc.scalar.activation(out=warm[:], in_=warm[:], func=ACT.Sigmoid)
+        nc.scalar.activation(out=warm[:], in_=warm[:], func=ACT.Exp)
 
         xq = const.tile([P, NPASS, B], U32, name="xq", align_bytes=64)
         xs = const.tile([P, NPASS, B], U8, name="xs", align_bytes=64)
@@ -84,42 +113,92 @@ def tile_slstmcell_kernel(tc, x_t, h_prev, c_prev, n_prev, W, R, b, out_0, out_1
         xh_w = xh[:].bitcast(F32)
 
         raws = {}
+        ones = {}
         gw = {}
         grouped = {}
         wq = {}
         ws = {}
 
-        def load_unit(u):
-            q, c = u // NPASS, u % NPASS
-            g, half = ORDER[q // 2], q % 2
+        def load_first_gate(c):
+            g = ORDER[0]
             src = W if c < 2 else R
             r0 = 512 * (c % 2)
-            c0 = g * H + half * HW
-            raw = rawp.tile([P, 4, HW], BF16, name="raw", tag="raw")
-            nc.sync.dma_start(
-                out=raw[:], in_=src[r0 : r0 + 512, c0 : c0 + HW].rearrange("(p j) w -> p j w", j=4)
-            )
-            raws[u] = raw
+            raw = rawp.tile([P, 4, H], BF16, name="raw", tag="raw")
+            cuts = FIRST_CUTS[c]
+            for k in range(cuts):
+                w0, w1 = k * H // cuts, (k + 1) * H // cuts
+                nc.sync.dma_start(
+                    out=raw[:, :, w0:w1], in_=src[r0 : r0 + 512, g * H + w0 : g * H + w1].rearrange("(p j) w -> p j w", j=4)
+                )
+            for half in range(2):
+                raws[NPASS * half + c] = raw[:, :, half * HW : (half + 1) * HW]
+
+        def load_pair(m):
+            raw = rawp.tile([P, 2, 4, HW], BF16, name="raw", tag="raw")
+            for k in range(2):
+                u = 2 * m + k
+                q, c = u // NPASS, u % NPASS
+                g, half = ORDER[q // 2], q % 2
+                src = W if c < 2 else R
+                r0 = 512 * (c % 2)
+                c0 = g * H + half * HW
+                nc.sync.dma_start(
+                    out=raw[:, k], in_=src[r0 : r0 + 512, c0 : c0 + HW].rearrange("(p j) w -> p j w", j=4)
+                )
+                raws[u] = raw[:, k]
 
         def new_tile(u):
-            if u not in gw:
-                grouped[u] = grp.tile([P, HW, 4], BF16, name="gr", tag="gr", align_bytes=64)
+            if u not in grouped:
+                if u in gw:
+                    grouped[u] = ggp.tile([P, HW, 4], BF16, name="gg", tag="gg", align_bytes=64)
+                else:
+                    grouped[u] = grp.tile([P, HW, 4], BF16, name="gr", tag="gr", align_bytes=64)
 
-        def gpsimd_copy(u):
-            gr = ggp.tile([P, HW, 4], BF16, name="gg", tag="gg", align_bytes=64)
-            grouped[u] = gr
-            if gw[u] > 0:
-                nc.gpsimd.tensor_scalar(
-                    out=gr[:, HW - gw[u] : HW, :],
-                    in0=raws[u][:, :, HW - gw[u] : HW].rearrange("p t w -> p w t"),
-                    scalar1=1.0,
-                    scalar2=0.0,
-                    op0=ALU.mult,
-                    op1=ALU.add,
+        def set_one(k):
+            one = onep.tile([P, 1], F32, name="one", tag="one")
+            ones[k] = one
+            nc.vector.memset(one[:], 1.0)
+
+        def gpsimd_copy(u, k):
+            new_tile(u)
+            nc.gpsimd.tensor_scalar(
+                out=grouped[u][:, HW - gw[u] : HW, :],
+                in0=raws[u][:, :, HW - gw[u] : HW].rearrange("p t w -> p w t"),
+                scalar1=ones[k][:, 0:1],
+                scalar2=0.0,
+                op0=ALU.mult,
+                op1=ALU.add,
+            )
+
+        def pe_cols(u):
+            return min(PE_COLS, (HW - gw.get(u, 0)) // P * P) if u in pe_at else ST_COLS if u in ST_UNITS else 0
+
+        banks = {}
+        pe_at = {}
+
+        def pe_group(u):
+            c0 = HW - gw.get(u, 0) - pe_cols(u)
+            banks[u] = []
+            for b in range(0, pe_cols(u), 256):
+                n = min(256, pe_cols(u) - b)
+                bank = tpp.tile([P, n, 4], BF16, name="idb", tag="tp")
+                banks[u].append((c0 + b, n, bank))
+                for k in range(0, n, P):
+                    nc.tensor.matmul(
+                        out=bank[:, k : k + P, :].rearrange("p c t -> p (c t)"), lhsT=identb[:], rhs=raws[u][:, :, c0 + b + k : c0 + b + k + P].rearrange("p t c -> p c t"),
+                        start=True, stop=True,
+                    )
+
+        def bank_copy(u):
+            new_tile(u)
+            for c0, n, bank in banks[u]:
+                nc.scalar.copy(
+                    out=grouped[u][:, c0 : c0 + n, :].rearrange("p c t -> p (c t)").bitcast(F32),
+                    in_=bank[:].rearrange("p c t -> p (c t)").bitcast(F32),
                 )
 
         def vector_cols(u):
-            return min(WA[u // NPASS], HW - gw.get(u, 0))
+            return min(WA[u // NPASS], HW - gw.get(u, 0) - pe_cols(u))
 
         def vector_copy(u):
             wa = vector_cols(u)
@@ -131,7 +210,7 @@ def tile_slstmcell_kernel(tc, x_t, h_prev, c_prev, n_prev, W, R, b, out_0, out_1
 
         def scalar_copy(u):
             wa = vector_cols(u)
-            sw = HW - gw.get(u, 0)
+            sw = HW - gw.get(u, 0) - pe_cols(u)
             if wa < sw:
                 nc.scalar.copy(
                     out=grouped[u][:, wa:sw, :].rearrange("p (c i) t -> p c t i", i=4),
@@ -180,12 +259,27 @@ def tile_slstmcell_kernel(tc, x_t, h_prev, c_prev, n_prev, W, R, b, out_0, out_1
             nc.vector.tensor_copy(out=bf32[:], in_=braw[:])
             pb = tpp.tile([P, BT, P], F32, name="pb", tag="tp")
             nc.tensor.transpose(out=pb[:, 0, :], in_=bf32[:], identity=ident[:])
-            nc.vector.tensor_copy(out=bias_sb[:, 0:24], in_=pb[:, 0, 0:24])
+            nc.vector.tensor_copy(out=bias_sb[:, 0:16], in_=pb[:, 0, 0:16])
             nc.vector.tensor_scalar(
-                out=bias_sb[:, 24:32], in0=pb[:, 0, 24:32], scalar1=0.5, scalar2=None, op0=ALU.mult
+                out=bias_sb[:, 16:32], in0=pb[:, 0, 16:32], scalar1=0.5, scalar2=None, op0=ALU.mult
             )
 
         accs = {}
+
+        def passes_by_tile(q):
+            for jl in range(4):
+                t = 4 * q + jl
+                accs[t] = accp.tile([P, B], F32, name="acc", tag="acc")
+                for c in range(NPASS):
+                    nc.tensor.matmul_mx(
+                        out=accs[t][:],
+                        lhsT=wq[q][:, c, jl * P : (jl + 1) * P].bitcast(FP8X4),
+                        lhsT_scale=ws[q][:, c, jl * P : (jl + 1) * P],
+                        rhs=xq[:, c, :].bitcast(FP8X4),
+                        rhs_scale=xs[:, c, :],
+                        start=(c == 0),
+                        stop=(c == NPASS - 1),
+                    )
 
         def passes(u):
             q, c = u // NPASS, u % NPASS
@@ -203,7 +297,7 @@ def tile_slstmcell_kernel(tc, x_t, h_prev, c_prev, n_prev, W, R, b, out_0, out_1
                     stop=(c == NPASS - 1),
                 )
 
-        FUNC = {GZ: ACT.Tanh, GI: ACT.Exp, GF: ACT.Sigmoid, GO: ACT.Tanh}
+        FUNC = {GZ: ACT.Tanh, GI: ACT.Exp, GF: ACT.Tanh, GO: ACT.Tanh}
 
         o_h = out_0.rearrange("(p t) h -> p t h", t=BT)
         o_c = out_1.rearrange("(p t) h -> p t h", t=BT)
@@ -215,16 +309,19 @@ def tile_slstmcell_kernel(tc, x_t, h_prev, c_prev, n_prev, W, R, b, out_0, out_1
         def halfcols(h):
             return slice(h * HW, (h + 1) * HW)
 
-        load_unit(0)
-        load_unit(1)
-        nc.sync.dma_start(out=xh[:, 0], in_=x_t.rearrange("(p t) k -> p t k", t=BT))
-        load_unit(2)
-        load_unit(3)
-        nc.sync.dma_start(out=xh[:, 1], in_=h_prev.rearrange("(p t) k -> p t k", t=BT))
-        for u in range(4, RAW_BUFS):
-            load_unit(u)
-        nc.sync.dma_start(out=cprev[:], in_=c_prev.rearrange("(p t) h -> p t h", t=BT))
-        nc.sync.dma_start(out=nprev[:], in_=n_prev.rearrange("(p t) h -> p t h", t=BT))
+        for what in FIRST_LOADS:
+            if what[0] == "f":
+                load_first_gate(int(what[1]))
+            elif what[0] == "u":
+                load_pair(int(what[1:]))
+            elif what == "x":
+                nc.sync.dma_start(out=xh[:, 0], in_=x_t.rearrange("(p t) k -> p t k", t=BT))
+            elif what == "h":
+                nc.sync.dma_start(out=xh[:, 1], in_=h_prev.rearrange("(p t) k -> p t k", t=BT))
+            elif what == "n":
+                nc.sync.dma_start(out=nprev[:], in_=n_prev.rearrange("(p t) h -> p t h", t=BT))
+            else:
+                nc.sync.dma_start(out=cprev[:], in_=c_prev.rearrange("(p t) h -> p t h", t=BT))
 
         cc = big.tile([P, BT, H], F32, name="cc", tag="big")
         nn = big.tile([P, BT, H], F32, name="nn", tag="big")
@@ -246,8 +343,11 @@ def tile_slstmcell_kernel(tc, x_t, h_prev, c_prev, n_prev, W, R, b, out_0, out_1
                     in_=accs[t][:],
                     func=FUNC[g],
                     bias=bias_sb[:, col : col + 1],
-                    scale=(0.5 if g == GO else 1.0),
+                    scale=(0.5 if g in (GF, GO) else 1.0),
                 )
+
+        def halve_n():
+            nc.vector.tensor_scalar(out=nprev[:], in0=nprev[:], scalar1=0.5, scalar2=None, op0=ALU.mult)
 
         def zmul(q):
             half = q % 2
@@ -261,19 +361,24 @@ def tile_slstmcell_kernel(tc, x_t, h_prev, c_prev, n_prev, W, R, b, out_0, out_1
                 nc.tensor.transpose(out=ps[:, bt, :], in_=gts[t][:, bt * P : (bt + 1) * P], identity=ident[:])
             pss[t] = ps
 
-        def rear_tile(t):
+        def rear_tile(t, part=None):
             g, j = ORDER[t // 8], t % 8
             js = cols(j)
             ps = pss[t]
             if g == GF:
-                nc.vector.tensor_tensor(out=cc[:, :, js], in0=ps[:], in1=cprev[:, :, js], op=ALU.mult)
-                nc.vector.tensor_tensor(out=nn[:, :, js], in0=ps[:], in1=nprev[:, :, js], op=ALU.mult)
+                for k, (dst, prev) in enumerate(((cc, cprev), (nn, nprev))):
+                    if part in (None, k):
+                        nc.vector.scalar_tensor_tensor(
+                            out=dst[:, :, js], in0=ps[:], scalar=1.0, in1=prev[:, :, js], op0=ALU.add, op1=ALU.mult
+                        )
             elif g == GI:
                 nc.vector.scalar_tensor_tensor(
                     out=nn[:, :, js], in0=ps[:], scalar=50.0, in1=nn[:, :, js], op0=ALU.min, op1=ALU.add
                 )
             elif g == GZ:
-                nc.vector.tensor_tensor(out=cc[:, :, js], in0=ps[:], in1=cc[:, :, js], op=ALU.add)
+                nc.vector.scalar_tensor_tensor(
+                    out=cc[:, :, js], in0=cc[:, :, js], scalar=0.5, in1=ps[:], op0=ALU.mult, op1=ALU.add
+                )
             else:
                 hh = late["hh"]
                 nc.vector.scalar_tensor_tensor(
@@ -287,8 +392,13 @@ def tile_slstmcell_kernel(tc, x_t, h_prev, c_prev, n_prev, W, R, b, out_0, out_1
 
         def rear_block(q):
             g, half = ORDER[q // 2], q % 2
-            for t in range(4 * q, 4 * q + 4):
-                rear_tile(t)
+            if g == GF and N_FIRST:
+                for part in (1, 0):
+                    for t in range(4 * q, 4 * q + 4):
+                        rear_tile(t, part)
+            else:
+                for t in range(4 * q, 4 * q + 4):
+                    rear_tile(t)
             hs = halfcols(half)
             if g == GI:
                 nc.sync.dma_start(out=o_n[:, :, hs], in_=nn[:, :, hs])
@@ -329,50 +439,77 @@ def tile_slstmcell_kernel(tc, x_t, h_prev, c_prev, n_prev, W, R, b, out_0, out_1
         def at(step, phase, fn, *args):
             plan.setdefault(step, []).append((phase, len(plan.get(step, ())), fn, args))
 
+        def pos(u):
+            return 2 * (u % NPASS) + u // NPASS if u < 8 else u + BUB
+
+        unit_at = {pos(u): u for u in range(NU)}
+
         def pass_step(u):
-            return max(u + (LAG_PASSES if u < NU - PROMPT_UNITS else 0), X_STEP + 1 + min(u, 3))
+            if 4 <= u < 8:
+                return pass_step(3) + 1
+            return max(pos(u) + (LAG_PASSES if u < NU - PROMPT_UNITS else 0), X_STEPS[u % NPASS] + 2 if u < 4 else 0)
+
+        def act_step(q):
+            return pass_step(4 * q + 3) + 1 + LAG_ACT[q]
 
         def rear_step(q):
-            return pass_step(4 * q + 3) + 2 + (1 if ORDER[q // 2] == GZ else 0)
+            return act_step(q) + 1 + LAG_REAR[q] + (1 if ORDER[q // 2] == GZ else 0)
 
-        chain = [rear_step(q) for q in range(6)] + [NU - 1]
-        for k, u in enumerate(chain):
-            if k == 0:
-                gw[u] = 0
-                at(u - LEAD_SCALAR, PH_NEW_TILE, gpsimd_copy, u)
-            else:
-                gw[u] = GW_TWO_READS if ORDER[(k - 1) // 2] == GF else GW_ONE_READ
-                at(chain[k - 1], PH_GPSIMD, gpsimd_copy, u)
+        for q in range(6):
+            r = rear_step(q)
+            at(r, PH_ONE, set_one, q)
+            nxt = min([v for v in range(NU) if pos(v) >= r + G_OFF] + [NU])
+            for k, width in enumerate(GW[q]):
+                if nxt + k < NU and width:
+                    gw[nxt + k] = width
+                    at(r, PH_REAR, gpsimd_copy, nxt + k, q)
+            nxt = min([v for v in range(NU) if pos(v) >= r + ID_TO] + [NU])
+            for k in range(ID_N[q]):
+                if nxt + k < NU:
+                    pe_at[nxt + k] = (r, k)
 
         for u in range(NU):
-            at(u - LEAD_SCALAR, PH_NEW_TILE, new_tile, u)
-            at(u - LEAD_SCALAR, PH_SCALAR_COPY, scalar_copy, u)
-            at(u - 1, PH_VECTOR_COPY, vector_copy, u)
-            if u + RAW_BUFS < NU:
-                at(u - 1, PH_LOAD, load_unit, u + RAW_BUFS)
-            at(u, PH_QUANT, quant, u)
-            at(pass_step(u), PH_PASSES, passes, u)
+            at(pos(u) - LEAD_SCALAR, PH_NEW_TILE, new_tile, u)
+            at(pos(u) - LEAD_SCALAR, PH_SCALAR_COPY, scalar_copy, u)
+            if u in ST_UNITS:
+                at(pos(u) - ST_LEAD, PH_TURN_X + 0.5, pe_group, u)
+                at(pos(u) - LEAD_SCALAR, PH_SCALAR_COPY - 0.5, bank_copy, u)
+            elif pe_cols(u):
+                r, k = pe_at[u]
+                at(r + ID_AT, PH_IDENT, pe_group, u)
+                at(min(pos(u) - 1, r + EV_AT + k // EV_PER), PH_SCALAR_COPY - 0.5, bank_copy, u)
+            at(pos(u) - 1, PH_VECTOR_COPY, vector_copy, u)
+            at(pos(u), PH_QUANT, quant, u)
+            if not 4 <= u < 8:
+                at(pass_step(u), PH_PASSES, passes, u)
+        at(pass_step(4), PH_PASSES, passes_by_tile, 1)
+        for m in range(RAW_BUFS, NU // 2):
+            k = m - RAW_BUFS
+            last = NPASS + k if k < 4 else 2 * k + 1
+            at(pos(last) - 1, PH_LOAD, load_pair, m)
         for c in range(NPASS):
-            at(X_STEP + c, PH_TURN_X, x_turn, 2 * c)
-            at(X_STEP + c, PH_TURN_X, x_turn, 2 * c + 1)
-            at(X_STEP + c, PH_SCALAR_FIRST, x_copy, 2 * c)
-            at(X_STEP + c, PH_SCALAR_FIRST, x_copy, 2 * c + 1)
-            at(X_STEP + c + 1, PH_QUANT_X, x_quant, c)
-        at(X_STEP + 2, PH_BIAS, bias_prep)
+            at(X_STEPS[c], PH_TURN_X, x_turn, 2 * c)
+            at(X_STEPS[c], PH_TURN_X, x_turn, 2 * c + 1)
+            at(X_STEPS[c], PH_SCALAR_FIRST, x_copy, 2 * c)
+            at(X_STEPS[c], PH_SCALAR_FIRST, x_copy, 2 * c + 1)
+            at(X_STEPS[c] + 1, PH_QUANT_X, x_quant, c)
+        at(BIAS_AT, -1, bias_prep)
+        at(rear_step(0), PH_HALVE, halve_n)
         for q in range(8):
             is_z = ORDER[q // 2] == GZ
-            a = pass_step(4 * q + 3) + 1
+            a = act_step(q)
             at(a, PH_SCALAR_FIRST, acts, q)
             if is_z:
                 at(a, PH_VECTOR_LAST, zmul, q)
             for j in range(4):
                 at(rear_step(q) - 1, PH_BACK, back, 4 * q + j)
-            at(rear_step(q) if q < 6 else NU + 1, PH_REAR, rear_block, q)
+
+            at(rear_step(q) if q < 6 else NU + BUB + 1, PH_REAR, rear_block, q)
             if is_z:
-                at(a + 3, PH_VECTOR_LAST, cdiv, q % 2)
+                at(a + LAG_CDIV, PH_VECTOR_LAST, cdiv, q % 2)
         n_done = rear_step(3)
-        at(n_done + 1, PH_SCALAR_FIRST, ars, 0)
-        at(n_done + 1, PH_SCALAR_FIRST, ars, 1)
+        at(n_done + LAG_ARS, PH_SCALAR_FIRST, ars, 0)
+        at(n_done + LAG_ARS, PH_SCALAR_FIRST, ars, 1)
         for h in range(2):
             at(n_done + LAG_SQUARE + h, PH_SQUARE, square, h)
             at(n_done + 1 + h, PH_VECTOR_LAST, sign, h)

@@ -24,7 +24,7 @@ ORDER = (GF, GI, GZ, GO)
 EPS = 1e-6
 FLOPS = 2 * 512 * 2048 * 4096
 
-WA = (256, 256, 32, 64, 352, 512, 0, 64)
+WA = (320, 320, 352, 0, 96, 512, 32, 64)
 PE_COLS = 256
 ID_AT = 0
 EV_AT = 1
@@ -38,22 +38,26 @@ BIAS_AT = -3
 N_FIRST = False
 LEAD_SCALAR = 2
 LEAD_GEV = 2
-LAG_ACT = (0, 3, 0, 1, 1, 1, 0, 0)
+LAG_ACT = (0, 0, 1, 1, 1, 1, 0, 0)
+ACT_STEP = {0: 8, 1: 10}
+REAR_STEP = {0: 10, 1: 12}
 LAG_REAR = (0, 0, 0, 0, 0, 0, 0, 0)
 LAG_PASSES = 1
 PROMPT_UNITS = 8
-BUB = 3
+BUB = 0
 RAW_BUFS = 4
 GR_BUFS = 6
 GG_BUFS = 3
-FIRST_CUTS = (1, 1, 1, 1)
-FIRST_LOADS = ("f0", "x", "f1", "h", "f2", "f3", "n", "c")
-X_STEPS = (0, 1, 2, 3)
-LAG_SQUARE = 3
-LAG_ARS = 1
-LAG_CDIV = 3
-GW = ((352,352), (352,352), (288,), (288,), (288,), (288,))
-G_OFF = 3
+FIRST_CUTS = (2,2,2,2)
+FIRST_LOADS = ("f0","x","f1","h","f2","f3","b","n","c")
+X_STEPS = (0, 1, 3, 4)
+SIGN_AT = (1, 2)
+SIGNED_AT = (4, 5)
+SQUARE_AT = (3, 4)
+ARS_AT = (1, 1)
+CDIV_AT = (3, 3)
+GW = ((320,), (320, 320), (288,), (288,), (288,), (288,))
+G_OFF = (3,3,3,3,3,3)
 
 PH_TURN_X = 0
 PH_NEW_TILE = 1
@@ -71,7 +75,7 @@ PH_BIAS = 11
 PH_SIGNED = 12
 PH_VECTOR_LAST = 13
 PH_BACK = 14
-PH_IDENT = 15.5
+PH_IDENT = 14.5
 PH_ONE = 8.5
 PH_PASSES = 15
 
@@ -133,8 +137,10 @@ def tile_slstmcell_kernel(tc, x_t, h_prev, c_prev, n_prev, W, R, b, out_0, out_1
             for half in range(2):
                 raws[NPASS * half + c] = raw[:, :, half * HW : (half + 1) * HW]
 
-        def load_pair(m):
-            raw = rawp.tile([P, 2, 4, HW], BF16, name="raw", tag="raw")
+        def load_pair(m, where=None):
+            raw = where
+            if raw is None:
+                raw = rawp.tile([P, 2, 4, HW], BF16, name="raw", tag="raw")
             for k in range(2):
                 u = 2 * m + k
                 q, c = u // NPASS, u % NPASS
@@ -312,8 +318,10 @@ def tile_slstmcell_kernel(tc, x_t, h_prev, c_prev, n_prev, W, R, b, out_0, out_1
         for what in FIRST_LOADS:
             if what[0] == "f":
                 load_first_gate(int(what[1]))
-            elif what[0] == "u":
-                load_pair(int(what[1:]))
+            elif what == "b":
+                rawb = big.tile([P, 2, 2, 4, HW], BF16, name="rawb", tag="big")
+                for m in (4, 5):
+                    load_pair(m, rawb[:, m - 4])
             elif what == "x":
                 nc.sync.dma_start(out=xh[:, 0], in_=x_t.rearrange("(p t) k -> p t k", t=BT))
             elif what == "h":
@@ -447,18 +455,22 @@ def tile_slstmcell_kernel(tc, x_t, h_prev, c_prev, n_prev, W, R, b, out_0, out_1
         def pass_step(u):
             if 4 <= u < 8:
                 return pass_step(3) + 1
-            return max(pos(u) + (LAG_PASSES if u < NU - PROMPT_UNITS else 0), X_STEPS[u % NPASS] + 2 if u < 4 else 0)
+            return max(pos(u) + (LAG_PASSES if u < NU - PROMPT_UNITS else 0), X_STEPS[u % NPASS] + 1 if u < 4 else 0)
 
         def act_step(q):
+            if q in ACT_STEP:
+                return ACT_STEP[q]
             return pass_step(4 * q + 3) + 1 + LAG_ACT[q]
 
         def rear_step(q):
+            if q in REAR_STEP:
+                return REAR_STEP[q]
             return act_step(q) + 1 + LAG_REAR[q] + (1 if ORDER[q // 2] == GZ else 0)
 
         for q in range(6):
             r = rear_step(q)
             at(r, PH_ONE, set_one, q)
-            nxt = min([v for v in range(NU) if pos(v) >= r + G_OFF] + [NU])
+            nxt = min([v for v in range(NU) if pos(v) >= r + G_OFF[q]] + [NU])
             for k, width in enumerate(GW[q]):
                 if nxt + k < NU and width:
                     gw[nxt + k] = width
@@ -483,9 +495,10 @@ def tile_slstmcell_kernel(tc, x_t, h_prev, c_prev, n_prev, W, R, b, out_0, out_1
             if not 4 <= u < 8:
                 at(pass_step(u), PH_PASSES, passes, u)
         at(pass_step(4), PH_PASSES, passes_by_tile, 1)
-        for m in range(RAW_BUFS, NU // 2):
-            k = m - RAW_BUFS
-            last = NPASS + k if k < 4 else 2 * k + 1
+        first = 6 if "b" in FIRST_LOADS else 4
+        for m in range(first, NU // 2):
+            k = m - first
+            last = NPASS + k if k < 4 else 2 * (m - 4) + 1
             at(pos(last) - 1, PH_LOAD, load_pair, m)
         for c in range(NPASS):
             at(X_STEPS[c], PH_TURN_X, x_turn, 2 * c)
@@ -506,14 +519,14 @@ def tile_slstmcell_kernel(tc, x_t, h_prev, c_prev, n_prev, W, R, b, out_0, out_1
 
             at(rear_step(q) if q < 6 else NU + BUB + 1, PH_REAR, rear_block, q)
             if is_z:
-                at(a + LAG_CDIV, PH_VECTOR_LAST, cdiv, q % 2)
+                at(a + CDIV_AT[q % 2], PH_VECTOR_LAST, cdiv, q % 2)
         n_done = rear_step(3)
-        at(n_done + LAG_ARS, PH_SCALAR_FIRST, ars, 0)
-        at(n_done + LAG_ARS, PH_SCALAR_FIRST, ars, 1)
+        at(n_done + ARS_AT[0], PH_SCALAR_FIRST, ars, 0)
+        at(n_done + ARS_AT[1], PH_SCALAR_FIRST, ars, 1)
         for h in range(2):
-            at(n_done + LAG_SQUARE + h, PH_SQUARE, square, h)
-            at(n_done + 1 + h, PH_VECTOR_LAST, sign, h)
-            at(n_done + LAG_SQUARE + 1 + h, PH_SIGNED, signed, h)
+            at(n_done + SQUARE_AT[h], PH_SQUARE, square, h)
+            at(n_done + SIGN_AT[h], PH_VECTOR_LAST, sign, h)
+            at(n_done + SIGNED_AT[h], PH_SIGNED, signed, h)
 
         ctx.enter_context(tc.manual_schedule(engines={ENG.PE, ENG.DVE, ENG.Activation, ENG.Pool}))
         for step in sorted(plan):

@@ -45,11 +45,15 @@ LAG_REAR = (0, 0, 0, 0, 0, 0, 0, 0)
 LAG_PASSES = 1
 PROMPT_UNITS = 8
 BUB = 0
+Q2_PASS = 0
+PASS1 = 8
+N_LAG = (0, 0)
+PIN_SP = False
 RAW_BUFS = 4
 GR_BUFS = 6
 GG_BUFS = 3
-FIRST_CUTS = (2,2,2,2)
-FIRST_LOADS = ("f0","x","f1","h","f2","f3","b","n","c")
+FIRST_CUTS = (1,1,1,1)
+FIRST_LOADS = ("f0","x","f1","h","f2","f3","b4","b5","n","c")
 X_STEPS = (0, 1, 3, 4)
 SIGN_AT = (1, 2)
 SIGNED_AT = (4, 5)
@@ -76,6 +80,7 @@ PH_SIGNED = 12
 PH_VECTOR_LAST = 13
 PH_BACK = 14
 PH_IDENT = 14.5
+PH_STORE = 9.5
 PH_ONE = 8.5
 PH_PASSES = 15
 
@@ -318,10 +323,11 @@ def tile_slstmcell_kernel(tc, x_t, h_prev, c_prev, n_prev, W, R, b, out_0, out_1
         for what in FIRST_LOADS:
             if what[0] == "f":
                 load_first_gate(int(what[1]))
-            elif what == "b":
-                rawb = big.tile([P, 2, 2, 4, HW], BF16, name="rawb", tag="big")
-                for m in (4, 5):
-                    load_pair(m, rawb[:, m - 4])
+            elif what[0] == "b":
+                m = int(what[1])
+                if m == 4:
+                    rawb = big.tile([P, 2, 2, 4, HW], BF16, name="rawb", tag="big")
+                load_pair(m, rawb[:, m - 4])
             elif what == "x":
                 nc.sync.dma_start(out=xh[:, 0], in_=x_t.rearrange("(p t) k -> p t k", t=BT))
             elif what == "h":
@@ -399,7 +405,7 @@ def tile_slstmcell_kernel(tc, x_t, h_prev, c_prev, n_prev, W, R, b, out_0, out_1
                     nc.sync.dma_start(out=o_h[:, :, hs], in_=hh[:, :, hs])
 
         def rear_block(q):
-            g, half = ORDER[q // 2], q % 2
+            g = ORDER[q // 2]
             if g == GF and N_FIRST:
                 for part in (1, 0):
                     for t in range(4 * q, 4 * q + 4):
@@ -407,11 +413,12 @@ def tile_slstmcell_kernel(tc, x_t, h_prev, c_prev, n_prev, W, R, b, out_0, out_1
             else:
                 for t in range(4 * q, 4 * q + 4):
                     rear_tile(t)
-            hs = halfcols(half)
-            if g == GI:
-                nc.sync.dma_start(out=o_n[:, :, hs], in_=nn[:, :, hs])
-            if g == GZ:
-                nc.sync.dma_start(out=o_c[:, :, hs], in_=cc[:, :, hs])
+
+        def store_n(h):
+            nc.sync.dma_start(out=o_n[:, :, halfcols(h)], in_=nn[:, :, halfcols(h)])
+
+        def store_c(h):
+            nc.sync.dma_start(out=o_c[:, :, halfcols(h)], in_=cc[:, :, halfcols(h)])
 
         def ars(h):
             if h == 0:
@@ -454,8 +461,8 @@ def tile_slstmcell_kernel(tc, x_t, h_prev, c_prev, n_prev, W, R, b, out_0, out_1
 
         def pass_step(u):
             if 4 <= u < 8:
-                return pass_step(3) + 1
-            return max(pos(u) + (LAG_PASSES if u < NU - PROMPT_UNITS else 0), X_STEPS[u % NPASS] + 1 if u < 4 else 0)
+                return PASS1
+            return max(pos(u) + (LAG_PASSES if u < NU - PROMPT_UNITS else 0), X_STEPS[u % NPASS] + 1 if u < 4 else Q2_PASS if 8 <= u < 12 else 0)
 
         def act_step(q):
             if q in ACT_STEP:
@@ -495,7 +502,7 @@ def tile_slstmcell_kernel(tc, x_t, h_prev, c_prev, n_prev, W, R, b, out_0, out_1
             if not 4 <= u < 8:
                 at(pass_step(u), PH_PASSES, passes, u)
         at(pass_step(4), PH_PASSES, passes_by_tile, 1)
-        first = 6 if "b" in FIRST_LOADS else 4
+        first = 6 if "b4" in FIRST_LOADS else 4
         for m in range(first, NU // 2):
             k = m - first
             last = NPASS + k if k < 4 else 2 * (m - 4) + 1
@@ -518,6 +525,10 @@ def tile_slstmcell_kernel(tc, x_t, h_prev, c_prev, n_prev, W, R, b, out_0, out_1
                 at(rear_step(q) - 1, PH_BACK, back, 4 * q + j)
 
             at(rear_step(q) if q < 6 else NU + BUB + 1, PH_REAR, rear_block, q)
+            if q in (2, 3):
+                at(rear_step(q) + N_LAG[q - 2], PH_STORE, store_n, q - 2)
+            if q in (4, 5):
+                at(rear_step(q), PH_STORE, store_c, q - 4)
             if is_z:
                 at(a + CDIV_AT[q % 2], PH_VECTOR_LAST, cdiv, q % 2)
         n_done = rear_step(3)
@@ -528,7 +539,7 @@ def tile_slstmcell_kernel(tc, x_t, h_prev, c_prev, n_prev, W, R, b, out_0, out_1
             at(n_done + SIGN_AT[h], PH_VECTOR_LAST, sign, h)
             at(n_done + SIGNED_AT[h], PH_SIGNED, signed, h)
 
-        ctx.enter_context(tc.manual_schedule(engines={ENG.PE, ENG.DVE, ENG.Activation, ENG.Pool}))
+        ctx.enter_context(tc.manual_schedule(engines={ENG.PE, ENG.DVE, ENG.Activation, ENG.Pool} | ({ENG.SP} if PIN_SP else set())))
         for step in sorted(plan):
             for phase, k, fn, args in sorted(plan[step], key=lambda it: (it[0], it[1])):
                 fn(*args)

from contextlib import ExitStack

import concourse.mybir as mybir
from concourse.masks import make_identity

F32 = mybir.dt.float32
BF16 = mybir.dt.bfloat16
U32 = mybir.dt.uint32
U8 = mybir.dt.uint8
FP8X4 = mybir.dt.float8_e4m3fn_x4
ACT = mybir.ActivationFunctionType
ALU = mybir.AluOpType
ENG = mybir.EngineType

P = 128
B = 512
H = 1024
HW = 512
BT = 4
NPASS = 4
NU = 32
GZ, GI, GF, GO = 0, 1, 2, 3
ORDER = (GF, GI, GZ, GO)
EPS = 1e-6
FLOPS = 2 * 512 * 2048 * 4096

WA = (320, 320, 352, 0, 96, 512, 32, 64)
PE_COLS = 256
ID_AT = 0
EV_AT = 1
ID_TO = 2
ID_N = (0,)*8
EV_PER = 2
ST_UNITS = ()
ST_COLS = 256
ST_LEAD = 2
BIAS_AT = -3
N_FIRST = False
LEAD_SCALAR = 2
LEAD_GEV = 2
LAG_ACT = (0, 0, 1, 1, 1, 1, 0, 0)
ACT_STEP = {0: 8, 1: 10}
REAR_STEP = {0: 10, 1: 12}
LAG_REAR = (0, 0, 0, 0, 0, 0, 0, 0)
LAG_PASSES = 1
PROMPT_UNITS = 8
BUB = 0
Q2_PASS = 0
PASS1 = 8
N_LAG = (0, 0)
PIN_SP = False
RAW_BUFS = 4
GR_BUFS = 6
GG_BUFS = 3
FIRST_CUTS = (1,1,1,1)
FIRST_LOADS = ("f0","x","f1","h","f2","f3","b4","b5","n","c")
X_STEPS = (0, 1, 3, 4)
SIGN_AT = (1, 2)
SIGNED_AT = (4, 5)
SQUARE_AT = (3, 4)
ARS_AT = (1, 1)
CDIV_AT = (3, 3)
GW = ((320,), (320, 320), (288,), (288,), (288,), (288,))
G_OFF = (3,3,3,3,3,3)

PH_TURN_X = 0
PH_NEW_TILE = 1
PH_SCALAR_FIRST = 2
PH_SQUARE = 3
PH_SCALAR_COPY = 4
PH_HALVE = 4.5
PH_VECTOR_COPY = 5
PH_LOAD = 6
PH_QUANT = 7
PH_GPSIMD = 8
PH_REAR = 9
PH_QUANT_X = 10
PH_BIAS = 11
PH_SIGNED = 12
PH_VECTOR_LAST = 13
PH_BACK = 14
PH_IDENT = 14.5
PH_STORE = 9.5
PH_ONE = 8.5
PH_PASSES = 15


def tile_slstmcell_kernel(tc, x_t, h_prev, c_prev, n_prev, W, R, b, out_0, out_1, out_2):
    nc = tc.nc
    with ExitStack() as ctx:
        const = ctx.enter_context(tc.tile_pool(name="const", bufs=1))
        big = ctx.enter_context(tc.tile_pool(name="big", bufs=5))
        gxp = ctx.enter_context(tc.tile_pool(name="gxp", bufs=2))
        rawp = ctx.enter_context(tc.tile_pool(name="rawp", bufs=RAW_BUFS))
        grp = ctx.enter_context(tc.tile_pool(name="grp", bufs=GR_BUFS))
        ggp = ctx.enter_context(tc.tile_pool(name="ggp", bufs=GG_BUFS))
        onep = ctx.enter_context(tc.tile_pool(name="onep", bufs=2))
        wqp = ctx.enter_context(tc.tile_pool(name="wqp", bufs=3))
        gtp = ctx.enter_context(tc.tile_pool(name="gtp", bufs=3))
        accp = ctx.enter_context(tc.psum_pool(name="accp", bufs=4))
        tpp = ctx.enter_context(tc.psum_pool(name="tpp", bufs=4))

        ident = const.tile([P, P], F32, name="ident")
        make_identity(nc, ident[:])
        identb = const.tile([P, P], BF16, name="identb")
        make_identity(nc, identb[:])
        braw = const.tile([P, P], BF16, name="braw")
        nc.scalar.dma_start(out=braw[0:32, :], in_=b.rearrange("(r c) -> r c", c=P))
        nc.vector.memset(braw[32:64, :], 0.0)
        nc.vector.memset(braw[64:128, :], 0.0)
        bias_sb = const.tile([P, 32], F32, name="bias_sb")
        warm = const.tile([P, 1], F32, name="warm")
        nc.vector.memset(warm[:], 0.0)
        nc.scalar.activation(out=warm[:], in_=warm[:], func=ACT.Exp)

        xq = const.tile([P, NPASS, B], U32, name="xq", align_bytes=64)
        xs = const.tile([P, NPASS, B], U8, name="xs", align_bytes=64)
        cprev = const.tile([P, BT, H], BF16, name="cprev")
        nprev = const.tile([P, BT, H], BF16, name="nprev")

        xh = big.tile([P, 2, BT, H], BF16, name="xh", tag="big")
        xh_w = xh[:].bitcast(F32)

        raws = {}
        ones = {}
        gw = {}
        grouped = {}
        wq = {}
        ws = {}

        def load_first_gate(c):
            g = ORDER[0]
            src = W if c < 2 else R
            r0 = 512 * (c % 2)
            raw = rawp.tile([P, 4, H], BF16, name="raw", tag="raw")
            cuts = FIRST_CUTS[c]
            for k in range(cuts):
                w0, w1 = k * H // cuts, (k + 1) * H // cuts
                nc.sync.dma_start(
                    out=raw[:, :, w0:w1], in_=src[r0 : r0 + 512, g * H + w0 : g * H + w1].rearrange("(p j) w -> p j w", j=4)
                )
            for half in range(2):
                raws[NPASS * half + c] = raw[:, :, half * HW : (half + 1) * HW]

        def load_pair(m, where=None):
            raw = where
            if raw is None:
                raw = rawp.tile([P, 2, 4, HW], BF16, name="raw", tag="raw")
            for k in range(2):
                u = 2 * m + k
                q, c = u // NPASS, u % NPASS
                g, half = ORDER[q // 2], q % 2
                src = W if c < 2 else R
                r0 = 512 * (c % 2)
                c0 = g * H + half * HW
                nc.sync.dma_start(
                    out=raw[:, k], in_=src[r0 : r0 + 512, c0 : c0 + HW].rearrange("(p j) w -> p j w", j=4)
                )
                raws[u] = raw[:, k]

        def new_tile(u):
            if u not in grouped:
                if u in gw:
                    grouped[u] = ggp.tile([P, HW, 4], BF16, name="gg", tag="gg", align_bytes=64)
                else:
                    grouped[u] = grp.tile([P, HW, 4], BF16, name="gr", tag="gr", align_bytes=64)

        def set_one(k):
            one = onep.tile([P, 1], F32, name="one", tag="one")
            ones[k] = one
            nc.vector.memset(one[:], 1.0)

        def gpsimd_copy(u, k):
            new_tile(u)
            nc.gpsimd.tensor_scalar(
                out=grouped[u][:, HW - gw[u] : HW, :],
                in0=raws[u][:, :, HW - gw[u] : HW].rearrange("p t w -> p w t"),
                scalar1=ones[k][:, 0:1],
                scalar2=0.0,
                op0=ALU.mult,
                op1=ALU.add,
            )

        def pe_cols(u):
            return min(PE_COLS, (HW - gw.get(u, 0)) // P * P) if u in pe_at else ST_COLS if u in ST_UNITS else 0

        banks = {}
        pe_at = {}

        def pe_group(u):
            c0 = HW - gw.get(u, 0) - pe_cols(u)
            banks[u] = []
            for b in range(0, pe_cols(u), 256):
                n = min(256, pe_cols(u) - b)
                bank = tpp.tile([P, n, 4], BF16, name="idb", tag="tp")
                banks[u].append((c0 + b, n, bank))
                for k in range(0, n, P):
                    nc.tensor.matmul(
                        out=bank[:, k : k + P, :].rearrange("p c t -> p (c t)"), lhsT=identb[:], rhs=raws[u][:, :, c0 + b + k : c0 + b + k + P].rearrange("p t c -> p c t"),
                        start=True, stop=True,
                    )

        def bank_copy(u):
            new_tile(u)
            for c0, n, bank in banks[u]:
                nc.scalar.copy(
                    out=grouped[u][:, c0 : c0 + n, :].rearrange("p c t -> p (c t)").bitcast(F32),
                    in_=bank[:].rearrange("p c t -> p (c t)").bitcast(F32),
                )

        def vector_cols(u):
            return min(WA[u // NPASS], HW - gw.get(u, 0) - pe_cols(u))

        def vector_copy(u):
            wa = vector_cols(u)
            if wa > 0:
                nc.vector.tensor_copy(
                    out=grouped[u][:, 0:wa, :].rearrange("p (c i) t -> p c t i", i=4),
                    in_=raws[u][:, :, 0:wa].rearrange("p t (c i) -> p c t i", i=4),
                )

        def scalar_copy(u):
            wa = vector_cols(u)
            sw = HW - gw.get(u, 0) - pe_cols(u)
            if wa < sw:
                nc.scalar.copy(
                    out=grouped[u][:, wa:sw, :].rearrange("p (c i) t -> p c t i", i=4),
                    in_=raws[u][:, :, wa:sw].rearrange("p t (c i) -> p c t i", i=4),
                )

        def quant(u):
            q, c = u // NPASS, u % NPASS
            if c == 0:
                wq[q] = wqp.tile([P, NPASS, HW], U32, name="wq", tag="wq", align_bytes=64)
                ws[q] = wqp.tile([P, NPASS, HW], U8, name="ws", tag="ws", align_bytes=64)
            nc.vector.quantize_mx(
                out=wq[q][:, c, :].bitcast(FP8X4),
                scales=ws[q][:, c, :],
                in_=grouped[u][:].rearrange("p w t -> p (w t)"),
            )

        xts = {}
        gxs = {}

        def x_turn(k):
            c, pair = k // 2, k % 2
            s, half = c // 2, c % 2
            xt = (accp if k < 4 else tpp).tile([P, 2, 256], F32, name="xt", tag=("acc" if k < 4 else "tp"))
            xts[k] = xt
            for bl in range(2):
                bt = 2 * pair + bl
                words = xh_w[:, s, bt, 256 * half : 256 * half + 256].rearrange("p (q u) -> p q u", u=2)
                for u in range(2):
                    nc.tensor.transpose(out=xt[:, u, bl * P : (bl + 1) * P], in_=words[:, :, u], identity=ident[:])

        def x_copy(k):
            c, pair = k // 2, k % 2
            if pair == 0:
                gxs[c] = gxp.tile([P, B, 4], BF16, name="gx", tag="gx", align_bytes=64)
            gx_w = gxs[c][:].bitcast(F32)
            nc.scalar.copy(out=gx_w[:, 256 * pair : 256 * pair + 256, :], in_=xts[k][:].rearrange("q u n -> q n u"))

        def x_quant(c):
            nc.vector.quantize_mx(
                out=xq[:, c, :].bitcast(FP8X4), scales=xs[:, c, :], in_=gxs[c][:].rearrange("p n t -> p (n t)")
            )

        def bias_prep():
            bf32 = const.tile([P, P], F32, name="bf32")
            nc.vector.tensor_copy(out=bf32[:], in_=braw[:])
            pb = tpp.tile([P, BT, P], F32, name="pb", tag="tp")
            nc.tensor.transpose(out=pb[:, 0, :], in_=bf32[:], identity=ident[:])
            nc.vector.tensor_copy(out=bias_sb[:, 0:16], in_=pb[:, 0, 0:16])
            nc.vector.tensor_scalar(
                out=bias_sb[:, 16:32], in0=pb[:, 0, 16:32], scalar1=0.5, scalar2=None, op0=ALU.mult
            )

        accs = {}

        def passes_by_tile(q):
            for jl in range(4):
                t = 4 * q + jl
                accs[t] = accp.tile([P, B], F32, name="acc", tag="acc")
                for c in range(NPASS):
                    nc.tensor.matmul_mx(
                        out=accs[t][:],
                        lhsT=wq[q][:, c, jl * P : (jl + 1) * P].bitcast(FP8X4),
                        lhsT_scale=ws[q][:, c, jl * P : (jl + 1) * P],
                        rhs=xq[:, c, :].bitcast(FP8X4),
                        rhs_scale=xs[:, c, :],
                        start=(c == 0),
                        stop=(c == NPASS - 1),
                    )

        def passes(u):
            q, c = u // NPASS, u % NPASS
            for jl in range(4):
                t = 4 * q + jl
                if c == 0:
                    accs[t] = accp.tile([P, B], F32, name="acc", tag="acc")
                nc.tensor.matmul_mx(
                    out=accs[t][:],
                    lhsT=wq[q][:, c, jl * P : (jl + 1) * P].bitcast(FP8X4),
                    lhsT_scale=ws[q][:, c, jl * P : (jl + 1) * P],
                    rhs=xq[:, c, :].bitcast(FP8X4),
                    rhs_scale=xs[:, c, :],
                    start=(c == 0),
                    stop=(c == NPASS - 1),
                )

        FUNC = {GZ: ACT.Tanh, GI: ACT.Exp, GF: ACT.Tanh, GO: ACT.Tanh}

        o_h = out_0.rearrange("(p t) h -> p t h", t=BT)
        o_c = out_1.rearrange("(p t) h -> p t h", t=BT)
        o_n = out_2.rearrange("(p t) h -> p t h", t=BT)

        def cols(j):
            return slice(j * P, (j + 1) * P)

        def halfcols(h):
            return slice(h * HW, (h + 1) * HW)

        for what in FIRST_LOADS:
            if what[0] == "f":
                load_first_gate(int(what[1]))
            elif what[0] == "b":
                m = int(what[1])
                if m == 4:
                    rawb = big.tile([P, 2, 2, 4, HW], BF16, name="rawb", tag="big")
                load_pair(m, rawb[:, m - 4])
            elif what == "x":
                nc.sync.dma_start(out=xh[:, 0], in_=x_t.rearrange("(p t) k -> p t k", t=BT))
            elif what == "h":
                nc.sync.dma_start(out=xh[:, 1], in_=h_prev.rearrange("(p t) k -> p t k", t=BT))
            elif what == "n":
                nc.sync.dma_start(out=nprev[:], in_=n_prev.rearrange("(p t) h -> p t h", t=BT))
            else:
                nc.sync.dma_start(out=cprev[:], in_=c_prev.rearrange("(p t) h -> p t h", t=BT))

        cc = big.tile([P, BT, H], F32, name="cc", tag="big")
        nn = big.tile([P, BT, H], F32, name="nn", tag="big")
        eT = big.tile([P, 8, B], F32, name="eT", tag="big")
        late = {}
        gts = {}
        gTs = {}
        pss = {}

        def acts(q):
            g = ORDER[q // 2]
            if g != GI:
                gTs[q] = gtp.tile([P, 4, B], F32, name="gT", tag="gT")
            for t in range(4 * q, 4 * q + 4):
                gts[t] = eT[:, t % 8, :] if g == GI else gTs[q][:, t % 4, :]
                col = g * 8 + t % 8
                nc.scalar.activation(
                    out=gts[t],
                    in_=accs[t][:],
                    func=FUNC[g],
                    bias=bias_sb[:, col : col + 1],
                    scale=(0.5 if g in (GF, GO) else 1.0),
                )

        def halve_n():
            nc.vector.tensor_scalar(out=nprev[:], in0=nprev[:], scalar1=0.5, scalar2=None, op0=ALU.mult)

        def zmul(q):
            half = q % 2
            nc.vector.scalar_tensor_tensor(
                out=gTs[q][:], in0=eT[:, 4 * half : 4 * half + 4, :], scalar=50.0, in1=gTs[q][:], op0=ALU.min, op1=ALU.mult
            )

        def back(t):
            ps = tpp.tile([P, BT, P], F32, name="ps", tag="tp")
            for bt in range(BT):
                nc.tensor.transpose(out=ps[:, bt, :], in_=gts[t][:, bt * P : (bt + 1) * P], identity=ident[:])
            pss[t] = ps

        def rear_tile(t, part=None):
            g, j = ORDER[t // 8], t % 8
            js = cols(j)
            ps = pss[t]
            if g == GF:
                for k, (dst, prev) in enumerate(((cc, cprev), (nn, nprev))):
                    if part in (None, k):
                        nc.vector.scalar_tensor_tensor(
                            out=dst[:, :, js], in0=ps[:], scalar=1.0, in1=prev[:, :, js], op0=ALU.add, op1=ALU.mult
                        )
            elif g == GI:
                nc.vector.scalar_tensor_tensor(
                    out=nn[:, :, js], in0=ps[:], scalar=50.0, in1=nn[:, :, js], op0=ALU.min, op1=ALU.add
                )
            elif g == GZ:
                nc.vector.scalar_tensor_tensor(
                    out=cc[:, :, js], in0=cc[:, :, js], scalar=0.5, in1=ps[:], op0=ALU.mult, op1=ALU.add
                )
            else:
                hh = late["hh"]
                nc.vector.scalar_tensor_tensor(
                    out=hh[:, :, js], in0=ps[:], scalar=1.0, in1=hh[:, :, js], op0=ALU.add, op1=ALU.mult
                )
                if j >= 6:
                    nc.sync.dma_start(out=o_h[:, :, js], in_=hh[:, :, js])
                elif j % 2 == 1:
                    hs = slice((j - 1) * P, (j + 1) * P)
                    nc.sync.dma_start(out=o_h[:, :, hs], in_=hh[:, :, hs])

        def rear_block(q):
            g = ORDER[q // 2]
            if g == GF and N_FIRST:
                for part in (1, 0):
                    for t in range(4 * q, 4 * q + 4):
                        rear_tile(t, part)
            else:
                for t in range(4 * q, 4 * q + 4):
                    rear_tile(t)

        def store_n(h):
            nc.sync.dma_start(out=o_n[:, :, halfcols(h)], in_=nn[:, :, halfcols(h)])

        def store_c(h):
            nc.sync.dma_start(out=o_c[:, :, halfcols(h)], in_=cc[:, :, halfcols(h)])

        def ars(h):
            if h == 0:
                late["sq"] = big.tile([P, BT, H], F32, name="sq", tag="big")
            nc.scalar.activation(
                out=late["sq"][:, :, halfcols(h)], in_=nn[:, :, halfcols(h)], func=ACT.Abs_reciprocal_sqrt, bias=EPS, scale=1.0
            )

        def sign(h):
            if h == 0:
                late["sg"] = big.tile([P, BT, H], F32, name="sg", tag="big")
            nc.vector.tensor_scalar(
                out=late["sg"][:, :, halfcols(h)], in0=nn[:, :, halfcols(h)], scalar1=-EPS, scalar2=0.5, op0=ALU.is_ge, op1=ALU.subtract
            )

        def square(h):
            sq = late["sq"]
            nc.scalar.activation(out=sq[:, :, halfcols(h)], in_=sq[:, :, halfcols(h)], func=ACT.Square)

        def signed(h):
            sq, sg = late["sq"], late["sg"]
            nc.vector.tensor_tensor(out=sq[:, :, halfcols(h)], in0=sq[:, :, halfcols(h)], in1=sg[:, :, halfcols(h)], op=ALU.mult)

        def cdiv(h):
            if h == 0:
                late["hh"] = big.tile([P, BT, H], F32, name="hh", tag="big")
            nc.vector.tensor_tensor(
                out=late["hh"][:, :, halfcols(h)], in0=cc[:, :, halfcols(h)], in1=late["sq"][:, :, halfcols(h)], op=ALU.mult
            )

        plan = {}

        def at(step, phase, fn, *args):
            plan.setdefault(step, []).append((phase, len(plan.get(step, ())), fn, args))

        def pos(u):
            return 2 * (u % NPASS) + u // NPASS if u < 8 else u + BUB

        unit_at = {pos(u): u for u in range(NU)}

        def pass_step(u):
            if 4 <= u < 8:
                return PASS1
            return max(pos(u) + (LAG_PASSES if u < NU - PROMPT_UNITS else 0), X_STEPS[u % NPASS] + 1 if u < 4 else Q2_PASS if 8 <= u < 12 else 0)

        def act_step(q):
            if q in ACT_STEP:
                return ACT_STEP[q]
            return pass_step(4 * q + 3) + 1 + LAG_ACT[q]

        def rear_step(q):
            if q in REAR_STEP:
                return REAR_STEP[q]
            return act_step(q) + 1 + LAG_REAR[q] + (1 if ORDER[q // 2] == GZ else 0)

        for q in range(6):
            r = rear_step(q)
            at(r, PH_ONE, set_one, q)
            nxt = min([v for v in range(NU) if pos(v) >= r + G_OFF[q]] + [NU])
            for k, width in enumerate(GW[q]):
                if nxt + k < NU and width:
                    gw[nxt + k] = width
                    at(r, PH_REAR, gpsimd_copy, nxt + k, q)
            nxt = min([v for v in range(NU) if pos(v) >= r + ID_TO] + [NU])
            for k in range(ID_N[q]):
                if nxt + k < NU:
                    pe_at[nxt + k] = (r, k)

        for u in range(NU):
            at(pos(u) - LEAD_SCALAR, PH_NEW_TILE, new_tile, u)
            at(pos(u) - LEAD_SCALAR, PH_SCALAR_COPY, scalar_copy, u)
            if u in ST_UNITS:
                at(pos(u) - ST_LEAD, PH_TURN_X + 0.5, pe_group, u)
                at(pos(u) - LEAD_SCALAR, PH_SCALAR_COPY - 0.5, bank_copy, u)
            elif pe_cols(u):
                r, k = pe_at[u]
                at(r + ID_AT, PH_IDENT, pe_group, u)
                at(min(pos(u) - 1, r + EV_AT + k // EV_PER), PH_SCALAR_COPY - 0.5, bank_copy, u)
            at(pos(u) - 1, PH_VECTOR_COPY, vector_copy, u)
            at(pos(u), PH_QUANT, quant, u)
            if not 4 <= u < 8:
                at(pass_step(u), PH_PASSES, passes, u)
        at(pass_step(4), PH_PASSES, passes_by_tile, 1)
        first = 6 if "b4" in FIRST_LOADS else 4
        for m in range(first, NU // 2):
            k = m - first
            last = NPASS + k if k < 4 else 2 * (m - 4) + 1
            at(pos(last) - 1, PH_LOAD, load_pair, m)
        for c in range(NPASS):
            at(X_STEPS[c], PH_TURN_X, x_turn, 2 * c)
            at(X_STEPS[c], PH_TURN_X, x_turn, 2 * c + 1)
            at(X_STEPS[c], PH_SCALAR_FIRST, x_copy, 2 * c)
            at(X_STEPS[c], PH_SCALAR_FIRST, x_copy, 2 * c + 1)
            at(X_STEPS[c] + 1, PH_QUANT_X, x_quant, c)
        at(BIAS_AT, -1, bias_prep)
        at(rear_step(0), PH_HALVE, halve_n)
        for q in range(8):
            is_z = ORDER[q // 2] == GZ
            a = act_step(q)
            at(a, PH_SCALAR_FIRST, acts, q)
            if is_z:
                at(a, PH_VECTOR_LAST, zmul, q)
            for j in range(4):
                at(rear_step(q) - 1, PH_BACK, back, 4 * q + j)

            at(rear_step(q) if q < 6 else NU + BUB + 1, PH_REAR, rear_block, q)
            if q in (2, 3):
                at(rear_step(q) + N_LAG[q - 2], PH_STORE, store_n, q - 2)
            if q in (4, 5):
                at(rear_step(q), PH_STORE, store_c, q - 4)
            if is_z:
                at(a + CDIV_AT[q % 2], PH_VECTOR_LAST, cdiv, q % 2)
        n_done = rear_step(3)
        at(n_done + ARS_AT[0], PH_SCALAR_FIRST, ars, 0)
        at(n_done + ARS_AT[1], PH_SCALAR_FIRST, ars, 1)
        for h in range(2):
            at(n_done + SQUARE_AT[h], PH_SQUARE, square, h)
            at(n_done + SIGN_AT[h], PH_VECTOR_LAST, sign, h)
            at(n_done + SIGNED_AT[h], PH_SIGNED, signed, h)

        ctx.enter_context(tc.manual_schedule(engines={ENG.PE, ENG.DVE, ENG.Activation, ENG.Pool} | ({ENG.SP} if PIN_SP else set())))
        for step in sorted(plan):
            for phase, k, fn, args in sorted(plan[step], key=lambda it: (it[0], it[1])):
                fn(*args)
